import numpy as np
import ml_dtypes

BF16 = ml_dtypes.bfloat16


def bf(x):
    return np.asarray(x, np.float32).astype(BF16)


def f32(x):
    return np.asarray(x, np.float32)


def f64(x):
    return np.asarray(x).astype(np.float64)


def striped(idx):
    return np.tile(idx.reshape(-1, 16).T, (8, 1))


NO, M, CA, C, S, N = 7, 128, 896, 1024, 1024, 256
KAPPA, SLOPE = 1.5, 0.2


def leaky(v):
    return np.where(v >= 0, v, SLOPE * v)


def setup_inputs():
    return {"base": f32(0.25 * np.random.random((C, S))), "adj": f32(np.random.random((CA, N)) < 0.5), "proc": f32(np.random.random((CA, N))), "el": f32(0.7 * np.random.standard_normal((NO, N))), "er": f32(0.5 * np.random.standard_normal((M, N))), "offs": striped(np.random.permutation(S)[:N])}


def reference(base, adj, proc, el, er, offs):
    idx = offs[:16].T.reshape(-1)
    A = f64(adj).reshape(NO, M, N)
    P = f64(proc).reshape(NO, M, N)
    R = f64(er)
    s = A * (f64(el)[:, None, :] + R[None, :, :]) + KAPPA * P
    w = np.concatenate([A * np.exp(leaky(s)), np.exp(leaky(2.0 * R))[None, :, :]], axis=0)
    den = w.sum(axis=0)
    alpha = w * (1.0 / den)[None, :, :]
    res = f64(base).copy()
    res[:, idx] = alpha.reshape(C, N)
    return res

@@ -1,0 +1,82 @@
+import concourse.mybir as mybir
+
+F32 = mybir.dt.float32
+U16 = mybir.dt.uint16
+ALU = mybir.AluOpType
+ACT = mybir.ActivationFunctionType
+
+P = 128
+OPS = 7
+ENTRIES = OPS + 1
+N = 256
+STORE = 1024
+KAPPA = 1.5
+SLOPE = 0.2
+DROP = 1.0e4
+
+
+def fold_entries(nc, pool, entries, op, name):
+    width = ENTRIES
+    while width > 1:
+        width //= 2
+        halved = pool.tile([P, width, N], F32, name=f"{name}{width}")
+        nc.vector.tensor_tensor(halved[:], entries[:, 0:width, :], entries[:, width : 2 * width, :], op)
+        entries = halved
+    return entries[:, 0, :]
+
+
+def tile_hgnnscheduler_kernel(tc, base, adj, proc, el, er, offs, out):
+    nc = tc.nc
+    base_blocks = base.rearrange("(n p) s -> n p s", p=P)
+    out_blocks = out.rearrange("(n p) s -> n p s", p=P)
+
+    with tc.tile_pool(name="held", bufs=1) as held:
+        offsets = held.tile([P, N // 16], U16, name="offsets")
+        nc.sync.dma_start(offsets[:], offs)
+        er_sb = held.tile([P, N], F32, name="er_sb")
+        nc.sync.dma_start(er_sb[:], er)
+        el_all = held.tile([P, OPS * N], F32, name="el_all")
+        nc.scalar.dma_start(el_all[:], el.rearrange("n j -> (n j)").partition_broadcast(P))
+        proc_sb = held.tile([P, OPS, N], F32, name="proc_sb")
+        nc.sync.dma_start(proc_sb[:], proc.rearrange("(n p) j -> p n j", p=P))
+        adj_sb = held.tile([P, OPS, N], F32, name="adj_sb")
+        nc.scalar.dma_start(adj_sb[:], adj.rearrange("(n p) j -> p n j", p=P))
+        windows = []
+        for n in range(ENTRIES):
+            window = held.tile([P, STORE], F32, name=f"window{n}")
+            queue = nc.sync if n % 2 == 0 else nc.scalar
+            queue.dma_start(window[:], base_blocks[n])
+            windows.append(window)
+
+        logit = held.tile([P, ENTRIES, N], F32, name="logit")
+        ops_logit = logit[:, 0:OPS, :]
+        score = held.tile([P, OPS, N], F32, name="score")
+        nc.vector.tensor_tensor(
+            score[:],
+            el_all[:].rearrange("p (n j) -> p n j", n=OPS),
+            er_sb[:].unsqueeze(1).to_broadcast([P, OPS, N]),
+            ALU.add,
+        )
+        nc.vector.scalar_tensor_tensor(score[:], proc_sb[:], KAPPA, score[:], ALU.mult, ALU.add)
+        nc.vector.scalar_tensor_tensor(ops_logit, score[:], SLOPE, score[:], ALU.mult, ALU.max)
+        drop = held.tile([P, OPS, N], F32, name="drop")
+        nc.vector.tensor_scalar(drop[:], adj_sb[:], DROP, -DROP, ALU.mult, ALU.add)
+        nc.vector.tensor_tensor(ops_logit, ops_logit, drop[:], ALU.add)
+        twice_er = held.tile([P, N], F32, name="twice_er")
+        nc.vector.tensor_scalar(twice_er[:], er_sb[:], 2.0, None, ALU.mult)
+        nc.vector.scalar_tensor_tensor(logit[:, OPS, :], twice_er[:], SLOPE, twice_er[:], ALU.mult, ALU.max)
+
+        top = fold_entries(nc, held, logit, ALU.max, "top")
+        nc.vector.tensor_tensor(
+            logit[:], logit[:], top.unsqueeze(1).to_broadcast([P, ENTRIES, N]), ALU.subtract
+        )
+        w = held.tile([P, ENTRIES, N], F32, name="w")
+        nc.scalar.activation(w[:], logit[:], ACT.Exp)
+        den = fold_entries(nc, held, w, ALU.add, "den")
+        inv_den = held.tile([P, N], F32, name="inv_den")
+        nc.vector.reciprocal(inv_den[:], den)
+
+        for n in range(ENTRIES):
+            nc.vector.tensor_tensor(windows[n][:].indirect(offsets[:]), w[:, n, :], inv_den[:], ALU.mult)
+            queue = nc.sync if n % 2 == 0 else nc.scalar
+            queue.dma_start(out_blocks[n], windows[n][:])

@@ -13,68 +13,108 @@ STORE = 1024
 KAPPA = 1.5
 SLOPE = 0.2
 DROP = 1.0e4
-
-
-def fold_entries(nc, pool, entries, op, name):
-    width = ENTRIES
-    while width > 1:
-        width //= 2
-        halved = pool.tile([P, width, N], F32, name=f"{name}{width}")
-        nc.vector.tensor_tensor(halved[:], entries[:, 0:width, :], entries[:, width : 2 * width, :], op)
-        entries = halved
-    return entries[:, 0, :]
+PAIR = 2
+PAIRS = ENTRIES // PAIR
 
 
 def tile_hgnnscheduler_kernel(tc, base, adj, proc, el, er, offs, out):
     nc = tc.nc
     base_blocks = base.rearrange("(n p) s -> n p s", p=P)
     out_blocks = out.rearrange("(n p) s -> n p s", p=P)
+    proc_by_machine = proc.rearrange("(n p) j -> p n j", p=P)
+    adj_by_machine = adj.rearrange("(n p) j -> p n j", p=P)
+    groups = [slice(first, min(first + PAIR, OPS)) for first in range(0, OPS, PAIR)]
 
     with tc.tile_pool(name="held", bufs=1) as held:
         offsets = held.tile([P, N // 16], U16, name="offsets")
         nc.sync.dma_start(offsets[:], offs)
         er_sb = held.tile([P, N], F32, name="er_sb")
         nc.sync.dma_start(er_sb[:], er)
-        el_all = held.tile([P, OPS * N], F32, name="el_all")
-        nc.scalar.dma_start(el_all[:], el.rearrange("n j -> (n j)").partition_broadcast(P))
+        el_sb = held.tile([P, OPS, N], F32, name="el_sb")
         proc_sb = held.tile([P, OPS, N], F32, name="proc_sb")
-        nc.sync.dma_start(proc_sb[:], proc.rearrange("(n p) j -> p n j", p=P))
         adj_sb = held.tile([P, OPS, N], F32, name="adj_sb")
-        nc.scalar.dma_start(adj_sb[:], adj.rearrange("(n p) j -> p n j", p=P))
+        for ops in groups:
+            nc.sync.dma_start(
+                el_sb[:, ops, :].rearrange("p n j -> p (n j)"),
+                el[ops, :].rearrange("n j -> (n j)").partition_broadcast(P),
+            )
+            nc.sync.dma_start(proc_sb[:, ops, :], proc_by_machine[:, ops, :])
+            nc.scalar.dma_start(adj_sb[:, ops, :], adj_by_machine[:, ops, :])
         windows = []
         for n in range(ENTRIES):
             window = held.tile([P, STORE], F32, name=f"window{n}")
-            queue = nc.sync if n % 2 == 0 else nc.scalar
-            queue.dma_start(window[:], base_blocks[n])
+            nc.sync.dma_start(window[:], base_blocks[n])
             windows.append(window)
 
-        logit = held.tile([P, ENTRIES, N], F32, name="logit")
-        ops_logit = logit[:, 0:OPS, :]
         score = held.tile([P, OPS, N], F32, name="score")
-        nc.vector.tensor_tensor(
-            score[:],
-            el_all[:].rearrange("p (n j) -> p n j", n=OPS),
-            er_sb[:].unsqueeze(1).to_broadcast([P, OPS, N]),
-            ALU.add,
-        )
-        nc.vector.scalar_tensor_tensor(score[:], proc_sb[:], KAPPA, score[:], ALU.mult, ALU.add)
-        nc.vector.scalar_tensor_tensor(ops_logit, score[:], SLOPE, score[:], ALU.mult, ALU.max)
         drop = held.tile([P, OPS, N], F32, name="drop")
-        nc.vector.tensor_scalar(drop[:], adj_sb[:], DROP, -DROP, ALU.mult, ALU.add)
-        nc.vector.tensor_tensor(ops_logit, ops_logit, drop[:], ALU.add)
-        twice_er = held.tile([P, N], F32, name="twice_er")
-        nc.vector.tensor_scalar(twice_er[:], er_sb[:], 2.0, None, ALU.mult)
-        nc.vector.scalar_tensor_tensor(logit[:, OPS, :], twice_er[:], SLOPE, twice_er[:], ALU.mult, ALU.max)
+        logit = held.tile([P, ENTRIES, N], F32, name="logit")
+        top_pair = held.tile([P, PAIR, N], F32, name="top_pair")
+        top = held.tile([P, N], F32, name="top")
 
-        top = fold_entries(nc, held, logit, ALU.max, "top")
-        nc.vector.tensor_tensor(
-            logit[:], logit[:], top.unsqueeze(1).to_broadcast([P, ENTRIES, N]), ALU.subtract
-        )
+        def add_el_er(ops):
+            nc.vector.tensor_tensor(
+                score[:, ops, :], el_sb[:, ops, :], er_sb[:].unsqueeze(1).to_broadcast(score[:, ops, :].shape), ALU.add
+            )
+
+        def add_proc(ops):
+            nc.vector.scalar_tensor_tensor(
+                score[:, ops, :], proc_sb[:, ops, :], KAPPA, score[:, ops, :], ALU.mult, ALU.add
+            )
+
+        def leaky(ops):
+            nc.vector.scalar_tensor_tensor(
+                score[:, ops, :], score[:, ops, :], SLOPE, score[:, ops, :], ALU.mult, ALU.max
+            )
+
+        def lower_forbidden(ops):
+            nc.vector.tensor_tensor(logit[:, ops, :], score[:, ops, :], drop[:, ops, :], ALU.add)
+
+        for ops in groups:
+            nc.scalar.activation(drop[:, ops, :], adj_sb[:, ops, :], ACT.Copy, bias=-DROP, scale=DROP)
+
+        twice_er = held.tile([P, N], F32, name="twice_er")
+        nc.vector.tensor_tensor(twice_er[:], er_sb[:], er_sb[:], ALU.add)
+        add_el_er(groups[0])
+        nc.vector.scalar_tensor_tensor(logit[:, OPS, :], twice_er[:], SLOPE, twice_er[:], ALU.mult, ALU.max)
+        add_proc(groups[0])
+        add_el_er(groups[1])
+        leaky(groups[0])
+        add_proc(groups[1])
+        lower_forbidden(groups[0])
+        leaky(groups[1])
+        add_el_er(groups[2])
+        lower_forbidden(groups[1])
+        add_proc(groups[2])
+        nc.vector.tensor_tensor(top_pair[:], logit[:, groups[0], :], logit[:, groups[1], :], ALU.max)
+        leaky(groups[2])
+        add_el_er(groups[3])
+        lower_forbidden(groups[2])
+        add_proc(groups[3])
+        nc.vector.tensor_tensor(top_pair[:], top_pair[:], logit[:, groups[2], :], ALU.max)
+        leaky(groups[3])
+        nc.vector.tensor_tensor(top[:], top_pair[:, 0, :], top_pair[:, 1, :], ALU.max)
+        lower_forbidden(groups[3])
+        nc.vector.tensor_tensor(top[:], top[:], logit[:, OPS, :], ALU.max)
+        nc.vector.tensor_tensor(top[:], top[:], logit[:, OPS - 1, :], ALU.max)
+
         w = held.tile([P, ENTRIES, N], F32, name="w")
-        nc.scalar.activation(w[:], logit[:], ACT.Exp)
-        den = fold_entries(nc, held, w, ALU.add, "den")
+        for k in range(PAIRS):
+            pair = slice(k * PAIR, (k + 1) * PAIR)
+            nc.vector.tensor_tensor(
+                logit[:, pair, :], logit[:, pair, :], top[:].unsqueeze(1).to_broadcast([P, PAIR, N]), ALU.subtract
+            )
+            nc.scalar.activation(w[:, pair, :], logit[:, pair, :], ACT.Exp)
+        den_pair = held.tile([P, PAIR, N], F32, name="den_pair")
+        nc.vector.tensor_tensor(den_pair[:], w[:, 0:2, :], w[:, 2:4, :], ALU.add)
+        nc.vector.tensor_tensor(den_pair[:], den_pair[:], w[:, 4:6, :], ALU.add)
+        den = held.tile([P, N], F32, name="den")
+        nc.vector.tensor_tensor(den[:], den_pair[:, 0, :], den_pair[:, 1, :], ALU.add)
+        den_last = held.tile([P, N], F32, name="den_last")
+        nc.vector.tensor_tensor(den_last[:], w[:, 6, :], w[:, 7, :], ALU.add)
+        nc.vector.tensor_tensor(den[:], den[:], den_last[:], ALU.add)
         inv_den = held.tile([P, N], F32, name="inv_den")
-        nc.vector.reciprocal(inv_den[:], den)
+        nc.vector.reciprocal(inv_den[:], den[:])
 
         for n in range(ENTRIES):
             nc.vector.tensor_tensor(windows[n][:].indirect(offsets[:]), w[:, n, :], inv_den[:], ALU.mult)

@@ -1,6 +1,8 @@
 import concourse.mybir as mybir
+from concourse.masks import make_identity
 
 F32 = mybir.dt.float32
+BF16 = mybir.dt.bfloat16
 U16 = mybir.dt.uint16
 ALU = mybir.AluOpType
 ACT = mybir.ActivationFunctionType
@@ -12,7 +14,7 @@ N = 256
 STORE = 1024
 KAPPA = 1.5
 SLOPE = 0.2
-DROP = 1.0e4
+DROP = 32768.0
 PAIR = 2
 PAIRS = ENTRIES // PAIR
 
@@ -25,76 +27,85 @@ def tile_hgnnscheduler_kernel(tc, base, adj, proc, el, er, offs, out):
     adj_by_machine = adj.rearrange("(n p) j -> p n j", p=P)
     groups = [slice(first, min(first + PAIR, OPS)) for first in range(0, OPS, PAIR)]
 
-    with tc.tile_pool(name="held", bufs=1) as held:
+    with (
+        tc.tile_pool(name="held", bufs=1) as held,
+        tc.psum_pool(name="banks", bufs=1) as banks,
+    ):
         offsets = held.tile([P, N // 16], U16, name="offsets")
         nc.sync.dma_start(offsets[:], offs)
         er_sb = held.tile([P, N], F32, name="er_sb")
         nc.sync.dma_start(er_sb[:], er)
-        el_sb = held.tile([P, OPS, N], F32, name="el_sb")
+        el_row = held.tile([1, OPS, N], F32, name="el_row")
+        nc.scalar.dma_start(el_row[:], el.rearrange("(a n) j -> a n j", a=1))
         proc_sb = held.tile([P, OPS, N], F32, name="proc_sb")
         adj_sb = held.tile([P, OPS, N], F32, name="adj_sb")
         for ops in groups:
-            nc.sync.dma_start(
-                el_sb[:, ops, :].rearrange("p n j -> p (n j)"),
-                el[ops, :].rearrange("n j -> (n j)").partition_broadcast(P),
-            )
-            nc.sync.dma_start(proc_sb[:, ops, :], proc_by_machine[:, ops, :])
             nc.scalar.dma_start(adj_sb[:, ops, :], adj_by_machine[:, ops, :])
+            nc.sync.dma_start(proc_sb[:, ops, :], proc_by_machine[:, ops, :])
         windows = []
         for n in range(ENTRIES):
             window = held.tile([P, STORE], F32, name=f"window{n}")
             nc.sync.dma_start(window[:], base_blocks[n])
             windows.append(window)
 
+        identity = held.tile([P, P], BF16, name="identity")
+        make_identity(nc, identity[:])
+        ones_row = held.tile([1, P], F32, name="ones_row")
+        nc.gpsimd.memset(ones_row[:], 1.0)
+
+        drop = held.tile([P, OPS, N], BF16, name="drop")
+        el_drop = []
+        for k, ops in enumerate(groups):
+            nc.scalar.activation(drop[:, ops, :], adj_sb[:, ops, :], ACT.Copy, bias=-DROP, scale=DROP)
+            bank = banks.tile(drop[:, ops, :].shape, F32, name=f"el_drop{k}")
+            nc.tensor.matmul(bank[:], ones_row[:], el_row[:, ops, :], start=True, stop=False)
+            nc.tensor.matmul(bank[:], identity[:], drop[:, ops, :], start=False, stop=True)
+            el_drop.append(bank)
+
         score = held.tile([P, OPS, N], F32, name="score")
-        drop = held.tile([P, OPS, N], F32, name="drop")
         logit = held.tile([P, ENTRIES, N], F32, name="logit")
         top_pair = held.tile([P, PAIR, N], F32, name="top_pair")
         top = held.tile([P, N], F32, name="top")
 
-        def add_el_er(ops):
-            nc.vector.tensor_tensor(
-                score[:, ops, :], el_sb[:, ops, :], er_sb[:].unsqueeze(1).to_broadcast(score[:, ops, :].shape), ALU.add
-            )
-
-        def add_proc(ops):
+        def add_proc_er(k):
+            ops = groups[k]
             nc.vector.scalar_tensor_tensor(
-                score[:, ops, :], proc_sb[:, ops, :], KAPPA, score[:, ops, :], ALU.mult, ALU.add
+                score[:, ops, :],
+                proc_sb[:, ops, :],
+                KAPPA,
+                er_sb[:].unsqueeze(1).to_broadcast(score[:, ops, :].shape),
+                ALU.mult,
+                ALU.add,
             )
 
-        def leaky(ops):
+        def add_el_drop(k):
+            ops = groups[k]
+            nc.vector.tensor_tensor(score[:, ops, :], score[:, ops, :], el_drop[k][:], ALU.add)
+
+        def leaky(k):
+            ops = groups[k]
             nc.vector.scalar_tensor_tensor(
-                score[:, ops, :], score[:, ops, :], SLOPE, score[:, ops, :], ALU.mult, ALU.max
+                logit[:, ops, :], score[:, ops, :], SLOPE, score[:, ops, :], ALU.mult, ALU.max
             )
-
-        def lower_forbidden(ops):
-            nc.vector.tensor_tensor(logit[:, ops, :], score[:, ops, :], drop[:, ops, :], ALU.add)
-
-        for ops in groups:
-            nc.scalar.activation(drop[:, ops, :], adj_sb[:, ops, :], ACT.Copy, bias=-DROP, scale=DROP)
 
         twice_er = held.tile([P, N], F32, name="twice_er")
         nc.vector.tensor_tensor(twice_er[:], er_sb[:], er_sb[:], ALU.add)
-        add_el_er(groups[0])
+        add_proc_er(0)
         nc.vector.scalar_tensor_tensor(logit[:, OPS, :], twice_er[:], SLOPE, twice_er[:], ALU.mult, ALU.max)
-        add_proc(groups[0])
-        add_el_er(groups[1])
-        leaky(groups[0])
-        add_proc(groups[1])
-        lower_forbidden(groups[0])
-        leaky(groups[1])
-        add_el_er(groups[2])
-        lower_forbidden(groups[1])
-        add_proc(groups[2])
+        add_proc_er(1)
+        add_el_drop(0)
+        add_proc_er(2)
+        leaky(0)
+        add_el_drop(1)
+        add_proc_er(3)
+        leaky(1)
+        add_el_drop(2)
         nc.vector.tensor_tensor(top_pair[:], logit[:, groups[0], :], logit[:, groups[1], :], ALU.max)
-        leaky(groups[2])
-        add_el_er(groups[3])
-        lower_forbidden(groups[2])
-        add_proc(groups[3])
+        leaky(2)
+        add_el_drop(3)
         nc.vector.tensor_tensor(top_pair[:], top_pair[:], logit[:, groups[2], :], ALU.max)
-        leaky(groups[3])
+        leaky(3)
         nc.vector.tensor_tensor(top[:], top_pair[:, 0, :], top_pair[:, 1, :], ALU.max)
-        lower_forbidden(groups[3])
         nc.vector.tensor_tensor(top[:], top[:], logit[:, OPS, :], ALU.max)
         nc.vector.tensor_tensor(top[:], top[:], logit[:, OPS - 1, :], ALU.max)
 

@@ -35,11 +35,14 @@ def tile_hgnnscheduler_kernel(tc, base, adj, proc, el, er, offs, out):
         nc.sync.dma_start(offsets[:], offs)
         er_sb = held.tile([P, N], F32, name="er_sb")
         nc.sync.dma_start(er_sb[:], er)
-        el_row = held.tile([1, OPS, N], F32, name="el_row")
-        nc.scalar.dma_start(el_row[:], el.rearrange("(a n) j -> a n j", a=1))
         proc_sb = held.tile([P, OPS, N], F32, name="proc_sb")
         adj_sb = held.tile([P, OPS, N], F32, name="adj_sb")
-        for ops in groups:
+        el_top = []
+        for k, ops in enumerate(groups):
+            padded = held.tile(proc_sb[:, ops, :].shape, F32, name=f"el_top{k}")
+            nc.vector.memset(padded[:], 0.0)
+            nc.sync.dma_start(padded[0:1, :, :], el[ops, :].rearrange("(a n) j -> a n j", a=1))
+            el_top.append(padded)
             nc.scalar.dma_start(adj_sb[:, ops, :], adj_by_machine[:, ops, :])
             nc.sync.dma_start(proc_sb[:, ops, :], proc_by_machine[:, ops, :])
         windows = []
@@ -50,15 +53,16 @@ def tile_hgnnscheduler_kernel(tc, base, adj, proc, el, er, offs, out):
 
         identity = held.tile([P, P], BF16, name="identity")
         make_identity(nc, identity[:])
-        ones_row = held.tile([1, P], F32, name="ones_row")
-        nc.gpsimd.memset(ones_row[:], 1.0)
+        first_row = held.tile([P, P], F32, name="first_row")
+        nc.gpsimd.memset(first_row[:], 0.0)
+        nc.gpsimd.memset(first_row[0:1, :], 1.0)
 
         drop = held.tile([P, OPS, N], BF16, name="drop")
         el_drop = []
         for k, ops in enumerate(groups):
             nc.scalar.activation(drop[:, ops, :], adj_sb[:, ops, :], ACT.Copy, bias=-DROP, scale=DROP)
             bank = banks.tile(drop[:, ops, :].shape, F32, name=f"el_drop{k}")
-            nc.tensor.matmul(bank[:], ones_row[:], el_row[:, ops, :], start=True, stop=False)
+            nc.tensor.matmul(bank[:], first_row[:], el_top[k][:], start=True, stop=False)
             nc.tensor.matmul(bank[:], identity[:], drop[:, ops, :], start=False, stop=True)
             el_drop.append(bank)
 

@@ -17,6 +17,7 @@ SLOPE = 0.2
 DROP = 32768.0
 PAIR = 2
 PAIRS = ENTRIES // PAIR
+WARMING_MATMULS = 4
 
 
 def tile_hgnnscheduler_kernel(tc, base, adj, proc, el, er, offs, out):
@@ -53,6 +54,11 @@ def tile_hgnnscheduler_kernel(tc, base, adj, proc, el, er, offs, out):
 
         identity = held.tile([P, P], BF16, name="identity")
         make_identity(nc, identity[:])
+        zeros = held.tile([P, PAIR * N], BF16, name="zeros")
+        nc.gpsimd.memset(zeros[:], 0.0)
+        unused = banks.tile([P, PAIR * N], F32, name="unused")
+        for repeat in range(WARMING_MATMULS):
+            nc.tensor.matmul(unused[:], identity[:], zeros[:], start=True, stop=True)
         first_row = held.tile([P, P], F32, name="first_row")
         nc.gpsimd.memset(first_row[:], 0.0)
         nc.gpsimd.memset(first_row[0:1, :], 1.0)

@@ -9,6 +9,7 @@ ACT = mybir.ActivationFunctionType
 
 P = 128
 OPS = 7
+SELF = OPS
 ENTRIES = OPS + 1
 N = 256
 STORE = 1024
@@ -16,8 +17,6 @@ KAPPA = 1.5
 SLOPE = 0.2
 DROP = 32768.0
 PAIR = 2
-PAIRS = ENTRIES // PAIR
-WARMING_MATMULS = 4
 
 
 def tile_hgnnscheduler_kernel(tc, base, adj, proc, el, er, offs, out):
@@ -26,7 +25,7 @@ def tile_hgnnscheduler_kernel(tc, base, adj, proc, el, er, offs, out):
     out_blocks = out.rearrange("(n p) s -> n p s", p=P)
     proc_by_machine = proc.rearrange("(n p) j -> p n j", p=P)
     adj_by_machine = adj.rearrange("(n p) j -> p n j", p=P)
-    groups = [slice(first, min(first + PAIR, OPS)) for first in range(0, OPS, PAIR)]
+    groups = [slice(0, 1)] + [slice(first, first + PAIR) for first in range(1, OPS, PAIR)]
 
     with (
         tc.tile_pool(name="held", bufs=1) as held,
@@ -54,11 +53,6 @@ def tile_hgnnscheduler_kernel(tc, base, adj, proc, el, er, offs, out):
 
         identity = held.tile([P, P], BF16, name="identity")
         make_identity(nc, identity[:])
-        zeros = held.tile([P, PAIR * N], BF16, name="zeros")
-        nc.gpsimd.memset(zeros[:], 0.0)
-        unused = banks.tile([P, PAIR * N], F32, name="unused")
-        for repeat in range(WARMING_MATMULS):
-            nc.tensor.matmul(unused[:], identity[:], zeros[:], start=True, stop=True)
         first_row = held.tile([P, P], F32, name="first_row")
         nc.gpsimd.memset(first_row[:], 0.0)
         nc.gpsimd.memset(first_row[0:1, :], 1.0)
@@ -74,8 +68,6 @@ def tile_hgnnscheduler_kernel(tc, base, adj, proc, el, er, offs, out):
 
         score = held.tile([P, OPS, N], F32, name="score")
         logit = held.tile([P, ENTRIES, N], F32, name="logit")
-        top_pair = held.tile([P, PAIR, N], F32, name="top_pair")
-        top = held.tile([P, N], F32, name="top")
 
         def add_proc_er(k):
             ops = groups[k]
@@ -98,10 +90,21 @@ def tile_hgnnscheduler_kernel(tc, base, adj, proc, el, er, offs, out):
                 logit[:, ops, :], score[:, ops, :], SLOPE, score[:, ops, :], ALU.mult, ALU.max
             )
 
+        top_ends = held.tile([P, N], F32, name="top_ends")
+        top_pair = held.tile([P, PAIR, N], F32, name="top_pair")
+        top_last = held.tile([P, N], F32, name="top_last")
+        top = held.tile([P, N], F32, name="top")
+
+        def top_of_ends():
+            nc.vector.tensor_tensor(top_ends[:], logit[:, 0, :], logit[:, SELF, :], ALU.max)
+
+        def top_of_middle():
+            nc.vector.tensor_tensor(top_pair[:], logit[:, groups[1], :], logit[:, groups[2], :], ALU.max)
+
         twice_er = held.tile([P, N], F32, name="twice_er")
         nc.vector.tensor_tensor(twice_er[:], er_sb[:], er_sb[:], ALU.add)
         add_proc_er(0)
-        nc.vector.scalar_tensor_tensor(logit[:, OPS, :], twice_er[:], SLOPE, twice_er[:], ALU.mult, ALU.max)
+        nc.vector.scalar_tensor_tensor(logit[:, SELF, :], twice_er[:], SLOPE, twice_er[:], ALU.mult, ALU.max)
         add_proc_er(1)
         add_el_drop(0)
         add_proc_er(2)
@@ -110,18 +113,19 @@ def tile_hgnnscheduler_kernel(tc, base, adj, proc, el, er, offs, out):
         add_proc_er(3)
         leaky(1)
         add_el_drop(2)
-        nc.vector.tensor_tensor(top_pair[:], logit[:, groups[0], :], logit[:, groups[1], :], ALU.max)
+        top_of_ends()
         leaky(2)
         add_el_drop(3)
-        nc.vector.tensor_tensor(top_pair[:], top_pair[:], logit[:, groups[2], :], ALU.max)
+        top_of_middle()
         leaky(3)
         nc.vector.tensor_tensor(top[:], top_pair[:, 0, :], top_pair[:, 1, :], ALU.max)
-        nc.vector.tensor_tensor(top[:], top[:], logit[:, OPS, :], ALU.max)
-        nc.vector.tensor_tensor(top[:], top[:], logit[:, OPS - 1, :], ALU.max)
+        nc.vector.tensor_tensor(top_last[:], logit[:, OPS - 2, :], logit[:, OPS - 1, :], ALU.max)
+        nc.vector.tensor_tensor(top[:], top[:], top_ends[:], ALU.max)
+        nc.vector.tensor_tensor(top[:], top[:], top_last[:], ALU.max)
 
         w = held.tile([P, ENTRIES, N], F32, name="w")
-        for k in range(PAIRS):
-            pair = slice(k * PAIR, (k + 1) * PAIR)
+        for first in range(0, ENTRIES, PAIR):
+            pair = slice(first, first + PAIR)
             nc.vector.tensor_tensor(
                 logit[:, pair, :], logit[:, pair, :], top[:].unsqueeze(1).to_broadcast([P, PAIR, N]), ALU.subtract
             )

@@ -12,11 +12,13 @@ OPS = 7
 SELF = OPS
 ENTRIES = OPS + 1
 N = 256
+HALVES = 2
+HALF = N // HALVES
 STORE = 1024
 KAPPA = 1.5
 SLOPE = 0.2
 DROP = 32768.0
-PAIR = 2
+QUAD = 4
 
 
 def tile_hgnnscheduler_kernel(tc, base, adj, proc, el, er, offs, out):
@@ -25,7 +27,8 @@ def tile_hgnnscheduler_kernel(tc, base, adj, proc, el, er, offs, out):
     out_blocks = out.rearrange("(n p) s -> n p s", p=P)
     proc_by_machine = proc.rearrange("(n p) j -> p n j", p=P)
     adj_by_machine = adj.rearrange("(n p) j -> p n j", p=P)
-    groups = [slice(0, 1)] + [slice(first, first + PAIR) for first in range(1, OPS, PAIR)]
+    op_groups = [slice(0, QUAD), slice(QUAD, OPS)]
+    entry_groups = [slice(0, QUAD), slice(QUAD, ENTRIES)]
 
     with (
         tc.tile_pool(name="held", bufs=1) as held,
@@ -35,111 +38,104 @@ def tile_hgnnscheduler_kernel(tc, base, adj, proc, el, er, offs, out):
         nc.sync.dma_start(offsets[:], offs)
         er_sb = held.tile([P, N], F32, name="er_sb")
         nc.sync.dma_start(er_sb[:], er)
-        proc_sb = held.tile([P, OPS, N], F32, name="proc_sb")
-        adj_sb = held.tile([P, OPS, N], F32, name="adj_sb")
-        el_top = []
-        for k, ops in enumerate(groups):
-            padded = held.tile(proc_sb[:, ops, :].shape, F32, name=f"el_top{k}")
-            nc.vector.memset(padded[:], 0.0)
-            nc.sync.dma_start(padded[0:1, :, :], el[ops, :].rearrange("(a n) j -> a n j", a=1))
-            el_top.append(padded)
-            nc.scalar.dma_start(adj_sb[:, ops, :], adj_by_machine[:, ops, :])
-            nc.sync.dma_start(proc_sb[:, ops, :], proc_by_machine[:, ops, :])
+        el_sb = held.tile([P, N], F32, name="el_sb")
+        nc.vector.memset(el_sb[:], 0.0)
+        nc.scalar.dma_start(el_sb[0:OPS, :], el)
+        proc_sb, adj_sb = [], []
+        for h in range(HALVES):
+            columns = slice(h * HALF, (h + 1) * HALF)
+            adj_half = held.tile([P, OPS, HALF], F32, name=f"adj_sb{h}")
+            proc_half = held.tile([P, OPS, HALF], F32, name=f"proc_sb{h}")
+            for ops in op_groups:
+                nc.scalar.dma_start(adj_half[:, ops, :], adj_by_machine[:, ops, columns])
+                nc.sync.dma_start(proc_half[:, ops, :], proc_by_machine[:, ops, columns])
+            adj_sb.append(adj_half)
+            proc_sb.append(proc_half)
         windows = []
         for n in range(ENTRIES):
             window = held.tile([P, STORE], F32, name=f"window{n}")
             nc.sync.dma_start(window[:], base_blocks[n])
             windows.append(window)
 
+        identity_f32 = held.tile([P, P], F32, name="identity_f32")
+        make_identity(nc, identity_f32[:])
         identity = held.tile([P, P], BF16, name="identity")
         make_identity(nc, identity[:])
-        first_row = held.tile([P, P], F32, name="first_row")
-        nc.gpsimd.memset(first_row[:], 0.0)
-        nc.gpsimd.memset(first_row[0:1, :], 1.0)
 
-        drop = held.tile([P, OPS, N], BF16, name="drop")
-        el_drop = []
-        for k, ops in enumerate(groups):
-            nc.scalar.activation(drop[:, ops, :], adj_sb[:, ops, :], ACT.Copy, bias=-DROP, scale=DROP)
-            bank = banks.tile(drop[:, ops, :].shape, F32, name=f"el_drop{k}")
-            nc.tensor.matmul(bank[:], first_row[:], el_top[k][:], start=True, stop=False)
-            nc.tensor.matmul(bank[:], identity[:], drop[:, ops, :], start=False, stop=True)
-            el_drop.append(bank)
-
-        score = held.tile([P, OPS, N], F32, name="score")
-        logit = held.tile([P, ENTRIES, N], F32, name="logit")
-
-        def add_proc_er(k):
-            ops = groups[k]
-            nc.vector.scalar_tensor_tensor(
-                score[:, ops, :],
-                proc_sb[:, ops, :],
-                KAPPA,
-                er_sb[:].unsqueeze(1).to_broadcast(score[:, ops, :].shape),
-                ALU.mult,
-                ALU.add,
-            )
-
-        def add_el_drop(k):
-            ops = groups[k]
-            nc.vector.tensor_tensor(score[:, ops, :], score[:, ops, :], el_drop[k][:], ALU.add)
-
-        def leaky(k):
-            ops = groups[k]
-            nc.vector.scalar_tensor_tensor(
-                logit[:, ops, :], score[:, ops, :], SLOPE, score[:, ops, :], ALU.mult, ALU.max
-            )
-
-        top_ends = held.tile([P, N], F32, name="top_ends")
-        top_pair = held.tile([P, PAIR, N], F32, name="top_pair")
-        top_last = held.tile([P, N], F32, name="top_last")
-        top = held.tile([P, N], F32, name="top")
-
-        def top_of_ends():
-            nc.vector.tensor_tensor(top_ends[:], logit[:, 0, :], logit[:, SELF, :], ALU.max)
-
-        def top_of_middle():
-            nc.vector.tensor_tensor(top_pair[:], logit[:, groups[1], :], logit[:, groups[2], :], ALU.max)
-
-        twice_er = held.tile([P, N], F32, name="twice_er")
-        nc.vector.tensor_tensor(twice_er[:], er_sb[:], er_sb[:], ALU.add)
-        add_proc_er(0)
-        nc.vector.scalar_tensor_tensor(logit[:, SELF, :], twice_er[:], SLOPE, twice_er[:], ALU.mult, ALU.max)
-        add_proc_er(1)
-        add_el_drop(0)
-        add_proc_er(2)
-        leaky(0)
-        add_el_drop(1)
-        add_proc_er(3)
-        leaky(1)
-        add_el_drop(2)
-        top_of_ends()
-        leaky(2)
-        add_el_drop(3)
-        top_of_middle()
-        leaky(3)
-        nc.vector.tensor_tensor(top[:], top_pair[:, 0, :], top_pair[:, 1, :], ALU.max)
-        nc.vector.tensor_tensor(top_last[:], logit[:, OPS - 2, :], logit[:, OPS - 1, :], ALU.max)
-        nc.vector.tensor_tensor(top[:], top[:], top_ends[:], ALU.max)
-        nc.vector.tensor_tensor(top[:], top[:], top_last[:], ALU.max)
-
+        drop = [held.tile([P, OPS, HALF], BF16, name=f"drop{h}") for h in range(HALVES)]
+        score = [held.tile([P, OPS, HALF], F32, name=f"score{h}") for h in range(HALVES)]
+        logit = [held.tile([P, ENTRIES, HALF], F32, name=f"logit{h}") for h in range(HALVES)]
         w = held.tile([P, ENTRIES, N], F32, name="w")
-        for first in range(0, ENTRIES, PAIR):
-            pair = slice(first, first + PAIR)
-            nc.vector.tensor_tensor(
-                logit[:, pair, :], logit[:, pair, :], top[:].unsqueeze(1).to_broadcast([P, PAIR, N]), ALU.subtract
-            )
-            nc.scalar.activation(w[:, pair, :], logit[:, pair, :], ACT.Exp)
-        den_pair = held.tile([P, PAIR, N], F32, name="den_pair")
-        nc.vector.tensor_tensor(den_pair[:], w[:, 0:2, :], w[:, 2:4, :], ALU.add)
-        nc.vector.tensor_tensor(den_pair[:], den_pair[:], w[:, 4:6, :], ALU.add)
-        den = held.tile([P, N], F32, name="den")
-        nc.vector.tensor_tensor(den[:], den_pair[:, 0, :], den_pair[:, 1, :], ALU.add)
-        den_last = held.tile([P, N], F32, name="den_last")
-        nc.vector.tensor_tensor(den_last[:], w[:, 6, :], w[:, 7, :], ALU.add)
-        nc.vector.tensor_tensor(den[:], den[:], den_last[:], ALU.add)
         inv_den = held.tile([P, N], F32, name="inv_den")
-        nc.vector.reciprocal(inv_den[:], den[:])
+
+        def own_entry(h):
+            er_half = er_sb[:, h * HALF : (h + 1) * HALF]
+            twice_er = held.tile([P, HALF], F32, name=f"twice_er{h}")
+            nc.vector.tensor_tensor(twice_er[:], er_half, er_half, ALU.add)
+            nc.vector.scalar_tensor_tensor(
+                logit[h][:, SELF, :], twice_er[:], SLOPE, twice_er[:], ALU.mult, ALU.max
+            )
+
+        def logits(h):
+            columns = slice(h * HALF, (h + 1) * HALF)
+            er_half = er_sb[:, columns]
+            el_drop = []
+            for g, ops in enumerate(op_groups):
+                nc.scalar.activation(drop[h][:, ops, :], adj_sb[h][:, ops, :], ACT.Copy, bias=-DROP, scale=DROP)
+                bank = banks.tile(drop[h][:, ops, :].shape, F32, name=f"el_drop{h}{g}")
+                for i, n in enumerate(range(ops.start, ops.stop)):
+                    row_n = identity_f32[:, n : n + 1].to_broadcast([P, P])
+                    nc.tensor.matmul(bank[:, i, :], row_n, el_sb[:, columns], start=(i == 0), stop=False)
+                nc.tensor.matmul(bank[:], identity[:], drop[h][:, ops, :], start=False, stop=True)
+                el_drop.append(bank)
+            for ops in op_groups:
+                nc.vector.scalar_tensor_tensor(
+                    score[h][:, ops, :],
+                    proc_sb[h][:, ops, :],
+                    KAPPA,
+                    er_half.unsqueeze(1).to_broadcast(score[h][:, ops, :].shape),
+                    ALU.mult,
+                    ALU.add,
+                )
+            for g, ops in enumerate(op_groups):
+                nc.vector.tensor_tensor(score[h][:, ops, :], score[h][:, ops, :], el_drop[g][:], ALU.add)
+                nc.vector.scalar_tensor_tensor(
+                    logit[h][:, ops, :], score[h][:, ops, :], SLOPE, score[h][:, ops, :], ALU.mult, ALU.max
+                )
+
+        def fold(h, values, op, what):
+            four = held.tile([P, QUAD, HALF], F32, name=f"{what}_four{h}")
+            nc.vector.tensor_tensor(four[:], values[:, 0:QUAD, :], values[:, QUAD:ENTRIES, :], op)
+            two = held.tile([P, 2, HALF], F32, name=f"{what}_two{h}")
+            nc.vector.tensor_tensor(two[:], four[:, 0:2, :], four[:, 2:4, :], op)
+            one = held.tile([P, HALF], F32, name=f"{what}_one{h}")
+            nc.vector.tensor_tensor(one[:], two[:, 0, :], two[:, 1, :], op)
+            return one
+
+        def exponentials(h):
+            top = fold(h, logit[h][:], ALU.max, "top")
+            columns = slice(h * HALF, (h + 1) * HALF)
+            for entries in entry_groups:
+                nc.vector.tensor_tensor(
+                    logit[h][:, entries, :],
+                    logit[h][:, entries, :],
+                    top[:].unsqueeze(1).to_broadcast([P, QUAD, HALF]),
+                    ALU.subtract,
+                )
+                nc.scalar.activation(w[:, entries, columns], logit[h][:, entries, :], ACT.Exp)
+
+        def denominator(h):
+            columns = slice(h * HALF, (h + 1) * HALF)
+            den = fold(h, w[:, :, columns], ALU.add, "den")
+            nc.vector.reciprocal(inv_den[:, columns], den[:])
+
+        for h in range(HALVES):
+            own_entry(h)
+        for h in range(HALVES):
+            logits(h)
+            exponentials(h)
+        for h in range(HALVES):
+            denominator(h)
 
         for n in range(ENTRIES):
             nc.vector.tensor_tensor(windows[n][:].indirect(offsets[:]), w[:, n, :], inv_den[:], ALU.mult)

@@ -6,6 +6,7 @@ BF16 = mybir.dt.bfloat16
 U16 = mybir.dt.uint16
 ALU = mybir.AluOpType
 ACT = mybir.ActivationFunctionType
+AXIS = mybir.AxisListType
 
 P = 128
 OPS = 7
@@ -19,6 +20,7 @@ KAPPA = 1.5
 SLOPE = 0.2
 DROP = 32768.0
 QUAD = 4
+AHEAD = 4
 
 
 def tile_hgnnscheduler_kernel(tc, base, adj, proc, el, er, offs, out):
@@ -124,20 +126,41 @@ def tile_hgnnscheduler_kernel(tc, base, adj, proc, el, er, offs, out):
                 )
                 nc.scalar.activation(w[:, entries, columns], logit[h][:, entries, :], ACT.Exp)
 
-        def denominator(h):
+        den = held.tile([P, N], F32, name="den")
+
+        def add_up(h):
             columns = slice(h * HALF, (h + 1) * HALF)
-            den = fold(h, w[:, :, columns], ALU.add, "den")
-            nc.vector.reciprocal(inv_den[:, columns], den[:])
+            nc.vector.tensor_reduce(den[:, columns], w[:, :, columns].rearrange("p n j -> p j n"), AXIS.X, ALU.add)
+
+        def invert(h):
+            columns = slice(h * HALF, (h + 1) * HALF)
+            nc.vector.reciprocal(inv_den[:, columns], den[:, columns])
+
+        def scatter_half(h, n):
+            columns = slice(h * HALF, (h + 1) * HALF)
+            piece = offsets[:, h * (HALF // 16) : (h + 1) * (HALF // 16)]
+            nc.vector.tensor_tensor(windows[n][:].indirect(piece), w[:, n, columns], inv_den[:, columns], ALU.mult)
+
+        def store(n):
+            queue = nc.sync if n % 2 == 0 else nc.scalar
+            queue.dma_start(out_blocks[n], windows[n][:])
 
         for h in range(HALVES):
             own_entry(h)
         for h in range(HALVES):
             logits(h)
             exponentials(h)
-        for h in range(HALVES):
-            denominator(h)
-
-        for n in range(ENTRIES):
+        add_up(0)
+        invert(0)
+        scatter_half(0, 0)
+        scatter_half(0, 1)
+        add_up(1)
+        scatter_half(0, 2)
+        invert(1)
+        scatter_half(0, 3)
+        for n in range(AHEAD):
+            scatter_half(1, n)
+            store(n)
+        for n in range(AHEAD, ENTRIES):
             nc.vector.tensor_tensor(windows[n][:].indirect(offsets[:]), w[:, n, :], inv_den[:], ALU.mult)
-            queue = nc.sync if n % 2 == 0 else nc.scalar
-            queue.dma_start(out_blocks[n], windows[n][:])
+            store(n)

@@ -6,7 +6,6 @@ BF16 = mybir.dt.bfloat16
 U16 = mybir.dt.uint16
 ALU = mybir.AluOpType
 ACT = mybir.ActivationFunctionType
-AXIS = mybir.AxisListType
 
 P = 128
 OPS = 7
@@ -29,6 +28,7 @@ def tile_hgnnscheduler_kernel(tc, base, adj, proc, el, er, offs, out):
     out_blocks = out.rearrange("(n p) s -> n p s", p=P)
     proc_by_machine = proc.rearrange("(n p) j -> p n j", p=P)
     adj_by_machine = adj.rearrange("(n p) j -> p n j", p=P)
+    el_row = el.rearrange("(a n) j -> a n j", a=1)
     op_groups = [slice(0, QUAD), slice(QUAD, OPS)]
     entry_groups = [slice(0, QUAD), slice(QUAD, ENTRIES)]
 
@@ -40,12 +40,13 @@ def tile_hgnnscheduler_kernel(tc, base, adj, proc, el, er, offs, out):
         nc.sync.dma_start(offsets[:], offs)
         er_sb = held.tile([P, N], F32, name="er_sb")
         nc.sync.dma_start(er_sb[:], er)
-        el_sb = held.tile([P, N], F32, name="el_sb")
-        nc.vector.memset(el_sb[:], 0.0)
-        nc.scalar.dma_start(el_sb[0:OPS, :], el)
-        proc_sb, adj_sb = [], []
+        proc_sb, adj_sb, el_top = [], [], []
         for h in range(HALVES):
             columns = slice(h * HALF, (h + 1) * HALF)
+            padded = held.tile([P, OPS, HALF], F32, name=f"el_top{h}")
+            nc.vector.memset(padded[:], 0.0)
+            nc.sync.dma_start(padded[0:1, :, :], el_row[:, :, columns])
+            el_top.append(padded)
             adj_half = held.tile([P, OPS, HALF], F32, name=f"adj_sb{h}")
             proc_half = held.tile([P, OPS, HALF], F32, name=f"proc_sb{h}")
             for ops in op_groups:
@@ -59,10 +60,11 @@ def tile_hgnnscheduler_kernel(tc, base, adj, proc, el, er, offs, out):
             nc.sync.dma_start(window[:], base_blocks[n])
             windows.append(window)
 
-        identity_f32 = held.tile([P, P], F32, name="identity_f32")
-        make_identity(nc, identity_f32[:])
         identity = held.tile([P, P], BF16, name="identity")
         make_identity(nc, identity[:])
+        first_row = held.tile([P, P], F32, name="first_row")
+        nc.gpsimd.memset(first_row[:], 0.0)
+        nc.gpsimd.memset(first_row[0:1, :], 1.0)
 
         drop = [held.tile([P, OPS, HALF], BF16, name=f"drop{h}") for h in range(HALVES)]
         score = [held.tile([P, OPS, HALF], F32, name=f"score{h}") for h in range(HALVES)]
@@ -85,9 +87,7 @@ def tile_hgnnscheduler_kernel(tc, base, adj, proc, el, er, offs, out):
             for g, ops in enumerate(op_groups):
                 nc.scalar.activation(drop[h][:, ops, :], adj_sb[h][:, ops, :], ACT.Copy, bias=-DROP, scale=DROP)
                 bank = banks.tile(drop[h][:, ops, :].shape, F32, name=f"el_drop{h}{g}")
-                for i, n in enumerate(range(ops.start, ops.stop)):
-                    row_n = identity_f32[:, n : n + 1].to_broadcast([P, P])
-                    nc.tensor.matmul(bank[:, i, :], row_n, el_sb[:, columns], start=(i == 0), stop=False)
+                nc.tensor.matmul(bank[:], first_row[:], el_top[h][:, ops, :], start=True, stop=False)
                 nc.tensor.matmul(bank[:], identity[:], drop[h][:, ops, :], start=False, stop=True)
                 el_drop.append(bank)
             for ops in op_groups:
@@ -126,11 +126,21 @@ def tile_hgnnscheduler_kernel(tc, base, adj, proc, el, er, offs, out):
                 )
                 nc.scalar.activation(w[:, entries, columns], logit[h][:, entries, :], ACT.Exp)
 
+        den_four = held.tile([P, QUAD, N], F32, name="den_four")
+        den_two = held.tile([P, 2, N], F32, name="den_two")
         den = held.tile([P, N], F32, name="den")
 
-        def add_up(h):
+        def add_to_four(h):
             columns = slice(h * HALF, (h + 1) * HALF)
-            nc.vector.tensor_reduce(den[:, columns], w[:, :, columns].rearrange("p n j -> p j n"), AXIS.X, ALU.add)
+            nc.vector.tensor_tensor(den_four[:, :, columns], w[:, 0:QUAD, columns], w[:, QUAD:ENTRIES, columns], ALU.add)
+
+        def add_to_two(h):
+            columns = slice(h * HALF, (h + 1) * HALF)
+            nc.vector.tensor_tensor(den_two[:, :, columns], den_four[:, 0:2, columns], den_four[:, 2:4, columns], ALU.add)
+
+        def add_to_one(h):
+            columns = slice(h * HALF, (h + 1) * HALF)
+            nc.vector.tensor_tensor(den[:, columns], den_two[:, 0, columns], den_two[:, 1, columns], ALU.add)
 
         def invert(h):
             columns = slice(h * HALF, (h + 1) * HALF)
@@ -150,14 +160,18 @@ def tile_hgnnscheduler_kernel(tc, base, adj, proc, el, er, offs, out):
         for h in range(HALVES):
             logits(h)
             exponentials(h)
-        add_up(0)
+        add_to_four(0)
+        add_to_two(0)
+        add_to_one(0)
         invert(0)
         scatter_half(0, 0)
         scatter_half(0, 1)
-        add_up(1)
+        add_to_four(1)
         scatter_half(0, 2)
-        invert(1)
+        add_to_two(1)
         scatter_half(0, 3)
+        add_to_one(1)
+        invert(1)
         for n in range(AHEAD):
             scatter_half(1, n)
             store(n)

@@ -65,6 +65,10 @@ def tile_hgnnscheduler_kernel(tc, base, adj, proc, el, er, offs, out):
         first_row = held.tile([P, P], F32, name="first_row")
         nc.gpsimd.memset(first_row[:], 0.0)
         nc.gpsimd.memset(first_row[0:1, :], 1.0)
+        identity_f32 = held.tile([P, P], F32, name="identity_f32")
+        nc.gpsimd.tensor_copy(identity_f32[:], identity[:])
+        minus_identity = held.tile([P, P], BF16, name="minus_identity")
+        nc.gpsimd.tensor_scalar_mul(minus_identity[:], identity[:], -1.0)
 
         drop = [held.tile([P, OPS, HALF], BF16, name=f"drop{h}") for h in range(HALVES)]
         score = [held.tile([P, OPS, HALF], F32, name=f"score{h}") for h in range(HALVES)]
@@ -80,16 +84,18 @@ def tile_hgnnscheduler_kernel(tc, base, adj, proc, el, er, offs, out):
                 logit[h][:, SELF, :], twice_er[:], SLOPE, twice_er[:], ALU.mult, ALU.max
             )
 
-        def logits(h):
-            columns = slice(h * HALF, (h + 1) * HALF)
-            er_half = er_sb[:, columns]
-            el_drop = []
+        el_drop = [[], []]
+
+        def el_and_drop(h):
             for g, ops in enumerate(op_groups):
                 nc.scalar.activation(drop[h][:, ops, :], adj_sb[h][:, ops, :], ACT.Copy, bias=-DROP, scale=DROP)
                 bank = banks.tile(drop[h][:, ops, :].shape, F32, name=f"el_drop{h}{g}")
                 nc.tensor.matmul(bank[:], first_row[:], el_top[h][:, ops, :], start=True, stop=False)
                 nc.tensor.matmul(bank[:], identity[:], drop[h][:, ops, :], start=False, stop=True)
-                el_drop.append(bank)
+                el_drop[h].append(bank)
+
+        def logits(h):
+            er_half = er_sb[:, h * HALF : (h + 1) * HALF]
             for ops in op_groups:
                 nc.vector.scalar_tensor_tensor(
                     score[h][:, ops, :],
@@ -100,31 +106,33 @@ def tile_hgnnscheduler_kernel(tc, base, adj, proc, el, er, offs, out):
                     ALU.add,
                 )
             for g, ops in enumerate(op_groups):
-                nc.vector.tensor_tensor(score[h][:, ops, :], score[h][:, ops, :], el_drop[g][:], ALU.add)
+                nc.vector.tensor_tensor(score[h][:, ops, :], score[h][:, ops, :], el_drop[h][g][:], ALU.add)
                 nc.vector.scalar_tensor_tensor(
                     logit[h][:, ops, :], score[h][:, ops, :], SLOPE, score[h][:, ops, :], ALU.mult, ALU.max
                 )
 
-        def fold(h, values, op, what):
-            four = held.tile([P, QUAD, HALF], F32, name=f"{what}_four{h}")
-            nc.vector.tensor_tensor(four[:], values[:, 0:QUAD, :], values[:, QUAD:ENTRIES, :], op)
-            two = held.tile([P, 2, HALF], F32, name=f"{what}_two{h}")
-            nc.vector.tensor_tensor(two[:], four[:, 0:2, :], four[:, 2:4, :], op)
-            one = held.tile([P, HALF], F32, name=f"{what}_one{h}")
-            nc.vector.tensor_tensor(one[:], two[:, 0, :], two[:, 1, :], op)
-            return one
-
         def exponentials(h):
-            top = fold(h, logit[h][:], ALU.max, "top")
+            shifted = []
+            for g, entries in enumerate(entry_groups):
+                bank = banks.tile([P, QUAD, HALF], F32, name=f"shifted{h}{g}")
+                nc.tensor.matmul(bank[:], identity_f32[:], logit[h][:, entries, :], start=True, stop=False)
+                shifted.append(bank)
+            top_four = held.tile([P, QUAD, HALF], F32, name=f"top_four{h}")
+            nc.vector.tensor_tensor(top_four[:], logit[h][:, 0:QUAD, :], logit[h][:, QUAD:ENTRIES, :], ALU.max)
+            top_two = held.tile([P, 2, HALF], F32, name=f"top_two{h}")
+            nc.vector.tensor_tensor(top_two[:], top_four[:, 0:2, :], top_four[:, 2:4, :], ALU.max)
+            top = held.tile([P, HALF], BF16, name=f"top{h}")
+            nc.vector.tensor_tensor(top[:], top_two[:, 0, :], top_two[:, 1, :], ALU.max)
             columns = slice(h * HALF, (h + 1) * HALF)
-            for entries in entry_groups:
-                nc.vector.tensor_tensor(
-                    logit[h][:, entries, :],
-                    logit[h][:, entries, :],
+            for g, entries in enumerate(entry_groups):
+                nc.tensor.matmul(
+                    shifted[g][:],
+                    minus_identity[:],
                     top[:].unsqueeze(1).to_broadcast([P, QUAD, HALF]),
-                    ALU.subtract,
+                    start=False,
+                    stop=True,
                 )
-                nc.scalar.activation(w[:, entries, columns], logit[h][:, entries, :], ACT.Exp)
+                nc.scalar.activation(w[:, entries, columns], shifted[g][:], ACT.Exp)
 
         den_four = held.tile([P, QUAD, N], F32, name="den_four")
         den_two = held.tile([P, 2, N], F32, name="den_two")
@@ -157,6 +165,8 @@ def tile_hgnnscheduler_kernel(tc, base, adj, proc, el, er, offs, out):
 
         for h in range(HALVES):
             own_entry(h)
+        for h in range(HALVES):
+            el_and_drop(h)
         for h in range(HALVES):
             logits(h)
             exponentials(h)

@@ -19,7 +19,6 @@ KAPPA = 1.5
 SLOPE = 0.2
 DROP = 32768.0
 QUAD = 4
-AHEAD = 4
 
 
 def tile_hgnnscheduler_kernel(tc, base, adj, proc, el, er, offs, out):
@@ -154,11 +153,6 @@ def tile_hgnnscheduler_kernel(tc, base, adj, proc, el, er, offs, out):
             columns = slice(h * HALF, (h + 1) * HALF)
             nc.vector.reciprocal(inv_den[:, columns], den[:, columns])
 
-        def scatter_half(h, n):
-            columns = slice(h * HALF, (h + 1) * HALF)
-            piece = offsets[:, h * (HALF // 16) : (h + 1) * (HALF // 16)]
-            nc.vector.tensor_tensor(windows[n][:].indirect(piece), w[:, n, columns], inv_den[:, columns], ALU.mult)
-
         def store(n):
             queue = nc.sync if n % 2 == 0 else nc.scalar
             queue.dma_start(out_blocks[n], windows[n][:])
@@ -170,21 +164,10 @@ def tile_hgnnscheduler_kernel(tc, base, adj, proc, el, er, offs, out):
         for h in range(HALVES):
             logits(h)
             exponentials(h)
-        add_to_four(0)
-        add_to_two(0)
-        add_to_one(0)
-        invert(0)
-        scatter_half(0, 0)
-        scatter_half(0, 1)
-        add_to_four(1)
-        scatter_half(0, 2)
-        add_to_two(1)
-        scatter_half(0, 3)
-        add_to_one(1)
-        invert(1)
-        for n in range(AHEAD):
-            scatter_half(1, n)
-            store(n)
-        for n in range(AHEAD, ENTRIES):
+        for step in (add_to_four, add_to_two, add_to_one, invert):
+            for h in range(HALVES):
+                step(h)
+
+        for n in range(ENTRIES):
             nc.vector.tensor_tensor(windows[n][:].indirect(offsets[:]), w[:, n, :], inv_den[:], ALU.mult)
             store(n)

@@ -89,9 +89,10 @@ def tile_hgnnscheduler_kernel(tc, base, adj, proc, el, er, offs, out):
             for g, ops in enumerate(op_groups):
                 nc.scalar.activation(drop[h][:, ops, :], adj_sb[h][:, ops, :], ACT.Copy, bias=-DROP, scale=DROP)
                 bank = banks.tile(drop[h][:, ops, :].shape, F32, name=f"el_drop{h}{g}")
-                nc.tensor.matmul(bank[:], first_row[:], el_top[h][:, ops, :], start=True, stop=False)
-                nc.tensor.matmul(bank[:], identity[:], drop[h][:, ops, :], start=False, stop=True)
+                nc.tensor.matmul(bank[:], identity[:], drop[h][:, ops, :], start=True, stop=False)
                 el_drop[h].append(bank)
+            for g, ops in enumerate(op_groups):
+                nc.tensor.matmul(el_drop[h][g][:], first_row[:], el_top[h][:, ops, :], start=False, stop=True)
 
         def logits(h):
             er_half = er_sb[:, h * HALF : (h + 1) * HALF]
@@ -116,9 +117,9 @@ def tile_hgnnscheduler_kernel(tc, base, adj, proc, el, er, offs, out):
                 bank = banks.tile([P, QUAD, HALF], F32, name=f"shifted{h}{g}")
                 nc.tensor.matmul(bank[:], identity_f32[:], logit[h][:, entries, :], start=True, stop=False)
                 shifted.append(bank)
-            top_four = held.tile([P, QUAD, HALF], F32, name=f"top_four{h}")
+            top_four = held.tile([P, QUAD, HALF], BF16, name=f"top_four{h}")
             nc.vector.tensor_tensor(top_four[:], logit[h][:, 0:QUAD, :], logit[h][:, QUAD:ENTRIES, :], ALU.max)
-            top_two = held.tile([P, 2, HALF], F32, name=f"top_two{h}")
+            top_two = held.tile([P, 2, HALF], BF16, name=f"top_two{h}")
             nc.vector.tensor_tensor(top_two[:], top_four[:, 0:2, :], top_four[:, 2:4, :], ALU.max)
             top = held.tile([P, HALF], BF16, name=f"top{h}")
             nc.vector.tensor_tensor(top[:], top_two[:, 0, :], top_two[:, 1, :], ALU.max)

@@ -39,20 +39,17 @@ def tile_hgnnscheduler_kernel(tc, base, adj, proc, el, er, offs, out):
         nc.sync.dma_start(offsets[:], offs)
         er_sb = held.tile([P, N], F32, name="er_sb")
         nc.sync.dma_start(er_sb[:], er)
-        proc_sb, adj_sb, el_top = [], [], []
-        for h in range(HALVES):
+        adj_sb = held.tile([P, OPS, N], F32, name="adj_sb")
+        proc_sb = held.tile([P, OPS, N], F32, name="proc_sb")
+        el_top = []
+        for h, ops in zip(range(HALVES), op_groups):
             columns = slice(h * HALF, (h + 1) * HALF)
             padded = held.tile([P, OPS, HALF], F32, name=f"el_top{h}")
             nc.vector.memset(padded[:], 0.0)
             nc.sync.dma_start(padded[0:1, :, :], el_row[:, :, columns])
             el_top.append(padded)
-            adj_half = held.tile([P, OPS, HALF], F32, name=f"adj_sb{h}")
-            proc_half = held.tile([P, OPS, HALF], F32, name=f"proc_sb{h}")
-            for ops in op_groups:
-                nc.scalar.dma_start(adj_half[:, ops, :], adj_by_machine[:, ops, columns])
-                nc.sync.dma_start(proc_half[:, ops, :], proc_by_machine[:, ops, columns])
-            adj_sb.append(adj_half)
-            proc_sb.append(proc_half)
+            nc.scalar.dma_start(adj_sb[:, ops, :], adj_by_machine[:, ops, :])
+            nc.sync.dma_start(proc_sb[:, ops, :], proc_by_machine[:, ops, :])
         windows = []
         for n in range(ENTRIES):
             window = held.tile([P, STORE], F32, name=f"window{n}")
@@ -86,8 +83,9 @@ def tile_hgnnscheduler_kernel(tc, base, adj, proc, el, er, offs, out):
         el_drop = [[], []]
 
         def el_and_drop(h):
+            columns = slice(h * HALF, (h + 1) * HALF)
             for g, ops in enumerate(op_groups):
-                nc.scalar.activation(drop[h][:, ops, :], adj_sb[h][:, ops, :], ACT.Copy, bias=-DROP, scale=DROP)
+                nc.scalar.activation(drop[h][:, ops, :], adj_sb[:, ops, columns], ACT.Copy, bias=-DROP, scale=DROP)
                 bank = banks.tile(drop[h][:, ops, :].shape, F32, name=f"el_drop{h}{g}")
                 nc.tensor.matmul(bank[:], identity[:], drop[h][:, ops, :], start=True, stop=False)
                 el_drop[h].append(bank)
@@ -95,11 +93,12 @@ def tile_hgnnscheduler_kernel(tc, base, adj, proc, el, er, offs, out):
                 nc.tensor.matmul(el_drop[h][g][:], first_row[:], el_top[h][:, ops, :], start=False, stop=True)
 
         def logits(h):
-            er_half = er_sb[:, h * HALF : (h + 1) * HALF]
+            columns = slice(h * HALF, (h + 1) * HALF)
+            er_half = er_sb[:, columns]
             for ops in op_groups:
                 nc.vector.scalar_tensor_tensor(
                     score[h][:, ops, :],
-                    proc_sb[h][:, ops, :],
+                    proc_sb[:, ops, columns],
                     KAPPA,
                     er_half.unsqueeze(1).to_broadcast(score[h][:, ops, :].shape),
                     ALU.mult,

@@ -19,6 +19,9 @@ KAPPA = 1.5
 SLOPE = 0.2
 DROP = 32768.0
 QUAD = 4
+QUARTER = N // 4
+PIECES = [slice(0, HALF), slice(HALF, HALF + QUARTER), slice(HALF + QUARTER, N)]
+GROUPS = [[slice(0, QUAD), slice(QUAD, ENTRIES)], [slice(0, ENTRIES)], [slice(0, ENTRIES)]]
 
 
 def tile_hgnnscheduler_kernel(tc, base, adj, proc, el, er, offs, out):
@@ -29,7 +32,6 @@ def tile_hgnnscheduler_kernel(tc, base, adj, proc, el, er, offs, out):
     adj_by_machine = adj.rearrange("(n p) j -> p n j", p=P)
     el_row = el.rearrange("(a n) j -> a n j", a=1)
     op_groups = [slice(0, QUAD), slice(QUAD, OPS)]
-    entry_groups = [slice(0, QUAD), slice(QUAD, ENTRIES)]
 
     with (
         tc.tile_pool(name="held", bufs=1) as held,
@@ -66,107 +68,108 @@ def tile_hgnnscheduler_kernel(tc, base, adj, proc, el, er, offs, out):
         minus_identity = held.tile([P, P], BF16, name="minus_identity")
         nc.gpsimd.tensor_scalar_mul(minus_identity[:], identity[:], -1.0)
 
-        drop = [held.tile([P, OPS, HALF], BF16, name=f"drop{h}") for h in range(HALVES)]
-        score = [held.tile([P, OPS, HALF], F32, name=f"score{h}") for h in range(HALVES)]
-        logit = [held.tile([P, ENTRIES, HALF], F32, name=f"logit{h}") for h in range(HALVES)]
+        pieces = range(len(PIECES))
+        width = [columns.stop - columns.start for columns in PIECES]
+        drop = [held.tile([P, OPS, width[i]], BF16, name=f"drop{i}") for i in pieces]
+        score = [held.tile([P, OPS, width[i]], F32, name=f"score{i}") for i in pieces]
+        logit = [held.tile([P, ENTRIES, width[i]], F32, name=f"logit{i}") for i in pieces]
         w = held.tile([P, ENTRIES, N], F32, name="w")
         inv_den = held.tile([P, N], F32, name="inv_den")
 
-        def own_entry(h):
-            er_half = er_sb[:, h * HALF : (h + 1) * HALF]
-            twice_er = held.tile([P, HALF], F32, name=f"twice_er{h}")
-            nc.vector.tensor_tensor(twice_er[:], er_half, er_half, ALU.add)
+        def operations(entries):
+            return slice(entries.start, min(entries.stop, OPS))
+
+        def own_entry(i):
+            er_piece = er_sb[:, PIECES[i]]
+            twice_er = held.tile([P, width[i]], F32, name=f"twice_er{i}")
+            nc.vector.tensor_tensor(twice_er[:], er_piece, er_piece, ALU.add)
             nc.vector.scalar_tensor_tensor(
-                logit[h][:, SELF, :], twice_er[:], SLOPE, twice_er[:], ALU.mult, ALU.max
+                logit[i][:, SELF, :], twice_er[:], SLOPE, twice_er[:], ALU.mult, ALU.max
             )
 
-        el_drop = [[], []]
+        el_drop = [[] for i in pieces]
 
-        def el_and_drop(h):
-            columns = slice(h * HALF, (h + 1) * HALF)
-            for g, ops in enumerate(op_groups):
-                nc.scalar.activation(drop[h][:, ops, :], adj_sb[:, ops, columns], ACT.Copy, bias=-DROP, scale=DROP)
-                bank = banks.tile(drop[h][:, ops, :].shape, F32, name=f"el_drop{h}{g}")
-                nc.tensor.matmul(bank[:], identity[:], drop[h][:, ops, :], start=True, stop=False)
-                el_drop[h].append(bank)
-            for g, ops in enumerate(op_groups):
-                nc.tensor.matmul(el_drop[h][g][:], first_row[:], el_top[h][:, ops, :], start=False, stop=True)
+        def el_and_drop(i):
+            columns = PIECES[i]
+            for g, entries in enumerate(GROUPS[i]):
+                ops = operations(entries)
+                nc.scalar.activation(drop[i][:, ops, :], adj_sb[:, ops, columns], ACT.Copy, bias=-DROP, scale=DROP)
+                bank = banks.tile(drop[i][:, ops, :].shape, F32, name=f"el_drop{i}{g}")
+                nc.tensor.matmul(bank[:], identity[:], drop[i][:, ops, :], start=True, stop=False)
+                el_drop[i].append(bank)
+            half = columns.start // HALF
+            in_half = slice(columns.start - half * HALF, columns.stop - half * HALF)
+            for g, entries in enumerate(GROUPS[i]):
+                el_piece = el_top[half][:, operations(entries), in_half]
+                nc.tensor.matmul(el_drop[i][g][:], first_row[:], el_piece, start=False, stop=True)
 
-        def logits(h):
-            columns = slice(h * HALF, (h + 1) * HALF)
-            er_half = er_sb[:, columns]
-            for ops in op_groups:
+        def logits(i):
+            columns = PIECES[i]
+            er_piece = er_sb[:, columns]
+            for entries in GROUPS[i]:
+                ops = operations(entries)
                 nc.vector.scalar_tensor_tensor(
-                    score[h][:, ops, :],
+                    score[i][:, ops, :],
                     proc_sb[:, ops, columns],
                     KAPPA,
-                    er_half.unsqueeze(1).to_broadcast(score[h][:, ops, :].shape),
+                    er_piece.unsqueeze(1).to_broadcast(score[i][:, ops, :].shape),
                     ALU.mult,
                     ALU.add,
                 )
-            for g, ops in enumerate(op_groups):
-                nc.vector.tensor_tensor(score[h][:, ops, :], score[h][:, ops, :], el_drop[h][g][:], ALU.add)
+            for g, entries in enumerate(GROUPS[i]):
+                ops = operations(entries)
+                nc.vector.tensor_tensor(score[i][:, ops, :], score[i][:, ops, :], el_drop[i][g][:], ALU.add)
                 nc.vector.scalar_tensor_tensor(
-                    logit[h][:, ops, :], score[h][:, ops, :], SLOPE, score[h][:, ops, :], ALU.mult, ALU.max
+                    logit[i][:, ops, :], score[i][:, ops, :], SLOPE, score[i][:, ops, :], ALU.mult, ALU.max
                 )
 
-        def exponentials(h):
+        def exponentials(i):
             shifted = []
-            for g, entries in enumerate(entry_groups):
-                bank = banks.tile([P, QUAD, HALF], F32, name=f"shifted{h}{g}")
-                nc.tensor.matmul(bank[:], identity_f32[:], logit[h][:, entries, :], start=True, stop=False)
+            for g, entries in enumerate(GROUPS[i]):
+                bank = banks.tile(logit[i][:, entries, :].shape, F32, name=f"shifted{i}{g}")
+                nc.tensor.matmul(bank[:], identity_f32[:], logit[i][:, entries, :], start=True, stop=False)
                 shifted.append(bank)
-            top_four = held.tile([P, QUAD, HALF], BF16, name=f"top_four{h}")
-            nc.vector.tensor_tensor(top_four[:], logit[h][:, 0:QUAD, :], logit[h][:, QUAD:ENTRIES, :], ALU.max)
-            top_two = held.tile([P, 2, HALF], BF16, name=f"top_two{h}")
+            top_four = held.tile([P, QUAD, width[i]], BF16, name=f"top_four{i}")
+            nc.vector.tensor_tensor(top_four[:], logit[i][:, 0:QUAD, :], logit[i][:, QUAD:ENTRIES, :], ALU.max)
+            top_two = held.tile([P, 2, width[i]], BF16, name=f"top_two{i}")
             nc.vector.tensor_tensor(top_two[:], top_four[:, 0:2, :], top_four[:, 2:4, :], ALU.max)
-            top = held.tile([P, HALF], BF16, name=f"top{h}")
+            top = held.tile([P, width[i]], BF16, name=f"top{i}")
             nc.vector.tensor_tensor(top[:], top_two[:, 0, :], top_two[:, 1, :], ALU.max)
-            columns = slice(h * HALF, (h + 1) * HALF)
-            for g, entries in enumerate(entry_groups):
-                nc.tensor.matmul(
-                    shifted[g][:],
-                    minus_identity[:],
-                    top[:].unsqueeze(1).to_broadcast([P, QUAD, HALF]),
-                    start=False,
-                    stop=True,
-                )
-                nc.scalar.activation(w[:, entries, columns], shifted[g][:], ACT.Exp)
+            for g, entries in enumerate(GROUPS[i]):
+                top_each = top[:].unsqueeze(1).to_broadcast(shifted[g][:].shape)
+                nc.tensor.matmul(shifted[g][:], minus_identity[:], top_each, start=False, stop=True)
+                nc.scalar.activation(w[:, entries, PIECES[i]], shifted[g][:], ACT.Exp)
 
         den_four = held.tile([P, QUAD, N], F32, name="den_four")
         den_two = held.tile([P, 2, N], F32, name="den_two")
         den = held.tile([P, N], F32, name="den")
 
-        def add_to_four(h):
-            columns = slice(h * HALF, (h + 1) * HALF)
+        def add_to_four(columns):
             nc.vector.tensor_tensor(den_four[:, :, columns], w[:, 0:QUAD, columns], w[:, QUAD:ENTRIES, columns], ALU.add)
 
-        def add_to_two(h):
-            columns = slice(h * HALF, (h + 1) * HALF)
+        def add_to_two(columns):
             nc.vector.tensor_tensor(den_two[:, :, columns], den_four[:, 0:2, columns], den_four[:, 2:4, columns], ALU.add)
 
-        def add_to_one(h):
-            columns = slice(h * HALF, (h + 1) * HALF)
+        def add_to_one(columns):
             nc.vector.tensor_tensor(den[:, columns], den_two[:, 0, columns], den_two[:, 1, columns], ALU.add)
 
-        def invert(h):
-            columns = slice(h * HALF, (h + 1) * HALF)
+        def invert(columns):
             nc.vector.reciprocal(inv_den[:, columns], den[:, columns])
 
         def store(n):
             queue = nc.sync if n % 2 == 0 else nc.scalar
             queue.dma_start(out_blocks[n], windows[n][:])
 
-        for h in range(HALVES):
-            own_entry(h)
-        for h in range(HALVES):
-            el_and_drop(h)
-        for h in range(HALVES):
-            logits(h)
-            exponentials(h)
+        for i in pieces:
+            own_entry(i)
+        for i in pieces:
+            el_and_drop(i)
+        for i in pieces:
+            logits(i)
+            exponentials(i)
         for step in (add_to_four, add_to_two, add_to_one, invert):
-            for h in range(HALVES):
-                step(h)
+            for columns in PIECES:
+                step(columns)
 
         for n in range(ENTRIES):
             nc.vector.tensor_tensor(windows[n][:].indirect(offsets[:]), w[:, n, :], inv_den[:], ALU.mult)

@@ -37,10 +37,10 @@ def tile_hgnnscheduler_kernel(tc, base, adj, proc, el, er, offs, out):
         tc.tile_pool(name="held", bufs=1) as held,
         tc.psum_pool(name="banks", bufs=1) as banks,
     ):
-        offsets = held.tile([P, N // 16], U16, name="offsets")
-        nc.sync.dma_start(offsets[:], offs)
         er_sb = held.tile([P, N], F32, name="er_sb")
         nc.sync.dma_start(er_sb[:], er)
+        offsets = held.tile([P, N // 16], U16, name="offsets")
+        nc.sync.dma_start(offsets[:], offs)
         adj_sb = held.tile([P, OPS, N], F32, name="adj_sb")
         proc_sb = held.tile([P, OPS, N], F32, name="proc_sb")
         el_top = []
@@ -58,15 +58,15 @@ def tile_hgnnscheduler_kernel(tc, base, adj, proc, el, er, offs, out):
             nc.sync.dma_start(window[:], base_blocks[n])
             windows.append(window)
 
+        identity_f32 = held.tile([P, P], F32, name="identity_f32")
+        make_identity(nc, identity_f32[:])
         identity = held.tile([P, P], BF16, name="identity")
-        make_identity(nc, identity[:])
+        nc.gpsimd.tensor_scalar_mul(identity[:], identity_f32[:], 1.0)
         first_row = held.tile([P, P], F32, name="first_row")
         nc.gpsimd.memset(first_row[:], 0.0)
         nc.gpsimd.memset(first_row[0:1, :], 1.0)
-        identity_f32 = held.tile([P, P], F32, name="identity_f32")
-        nc.gpsimd.tensor_copy(identity_f32[:], identity[:])
         minus_identity = held.tile([P, P], BF16, name="minus_identity")
-        nc.gpsimd.tensor_scalar_mul(minus_identity[:], identity[:], -1.0)
+        nc.gpsimd.tensor_scalar_mul(minus_identity[:], identity_f32[:], -1.0)
 
         pieces = range(len(PIECES))
         width = [columns.stop - columns.start for columns in PIECES]
@@ -87,48 +87,69 @@ def tile_hgnnscheduler_kernel(tc, base, adj, proc, el, er, offs, out):
                 logit[i][:, SELF, :], twice_er[:], SLOPE, twice_er[:], ALU.mult, ALU.max
             )
 
-        el_drop = [[] for i in pieces]
+        er_in_bank = [(0, 1)]
+        banks_of = [[] for i in pieces]
+
+        def open_banks(i):
+            for g, entries in enumerate(GROUPS[i]):
+                shape = score[i][:, operations(entries), :].shape
+                bank = banks.tile(shape, F32, name=f"sum{i}{g}")
+                if (i, g) in er_in_bank:
+                    er_each = er_sb[:, PIECES[i]].unsqueeze(1).to_broadcast(shape)
+                    nc.tensor.matmul(bank[:], identity_f32[:], er_each, start=True, stop=False)
+                banks_of[i].append(bank)
 
         def el_and_drop(i):
             columns = PIECES[i]
             for g, entries in enumerate(GROUPS[i]):
                 ops = operations(entries)
                 nc.scalar.activation(drop[i][:, ops, :], adj_sb[:, ops, columns], ACT.Copy, bias=-DROP, scale=DROP)
-                bank = banks.tile(drop[i][:, ops, :].shape, F32, name=f"el_drop{i}{g}")
-                nc.tensor.matmul(bank[:], identity[:], drop[i][:, ops, :], start=True, stop=False)
-                el_drop[i].append(bank)
+                first = (i, g) not in er_in_bank
+                nc.tensor.matmul(banks_of[i][g][:], identity[:], drop[i][:, ops, :], start=first, stop=False)
             half = columns.start // HALF
             in_half = slice(columns.start - half * HALF, columns.stop - half * HALF)
             for g, entries in enumerate(GROUPS[i]):
                 el_piece = el_top[half][:, operations(entries), in_half]
-                nc.tensor.matmul(el_drop[i][g][:], first_row[:], el_piece, start=False, stop=True)
+                nc.tensor.matmul(banks_of[i][g][:], first_row[:], el_piece, start=False, stop=True)
 
         def logits(i):
             columns = PIECES[i]
             er_piece = er_sb[:, columns]
-            for entries in GROUPS[i]:
-                ops = operations(entries)
-                nc.vector.scalar_tensor_tensor(
-                    score[i][:, ops, :],
-                    proc_sb[:, ops, columns],
-                    KAPPA,
-                    er_piece.unsqueeze(1).to_broadcast(score[i][:, ops, :].shape),
-                    ALU.mult,
-                    ALU.add,
-                )
             for g, entries in enumerate(GROUPS[i]):
                 ops = operations(entries)
-                nc.vector.tensor_tensor(score[i][:, ops, :], score[i][:, ops, :], el_drop[i][g][:], ALU.add)
+                if (i, g) not in er_in_bank:
+                    nc.vector.scalar_tensor_tensor(
+                        score[i][:, ops, :],
+                        proc_sb[:, ops, columns],
+                        KAPPA,
+                        er_piece.unsqueeze(1).to_broadcast(score[i][:, ops, :].shape),
+                        ALU.mult,
+                        ALU.add,
+                    )
+            for g, entries in enumerate(GROUPS[i]):
+                ops = operations(entries)
+                bank = banks_of[i][g]
+                if (i, g) in er_in_bank:
+                    nc.vector.scalar_tensor_tensor(
+                        score[i][:, ops, :], proc_sb[:, ops, columns], KAPPA, bank[:], ALU.mult, ALU.add
+                    )
+                else:
+                    nc.vector.tensor_tensor(score[i][:, ops, :], score[i][:, ops, :], bank[:], ALU.add)
                 nc.vector.scalar_tensor_tensor(
                     logit[i][:, ops, :], score[i][:, ops, :], SLOPE, score[i][:, ops, :], ALU.mult, ALU.max
                 )
 
         def exponentials(i):
+            on_vector = i == 1
             shifted = []
             for g, entries in enumerate(GROUPS[i]):
-                bank = banks.tile(logit[i][:, entries, :].shape, F32, name=f"shifted{i}{g}")
-                nc.tensor.matmul(bank[:], identity_f32[:], logit[i][:, entries, :], start=True, stop=False)
-                shifted.append(bank)
+                if on_vector:
+                    below_top = held.tile(logit[i][:, entries, :].shape, F32, name=f"below_top{i}{g}")
+                    shifted.append(below_top)
+                else:
+                    bank = banks.tile(logit[i][:, entries, :].shape, F32, name=f"shifted{i}{g}")
+                    nc.tensor.matmul(bank[:], identity_f32[:], logit[i][:, entries, :], start=True, stop=False)
+                    shifted.append(bank)
             top_four = held.tile([P, QUAD, width[i]], BF16, name=f"top_four{i}")
             nc.vector.tensor_tensor(top_four[:], logit[i][:, 0:QUAD, :], logit[i][:, QUAD:ENTRIES, :], ALU.max)
             top_two = held.tile([P, 2, width[i]], BF16, name=f"top_two{i}")
@@ -137,7 +158,10 @@ def tile_hgnnscheduler_kernel(tc, base, adj, proc, el, er, offs, out):
             nc.vector.tensor_tensor(top[:], top_two[:, 0, :], top_two[:, 1, :], ALU.max)
             for g, entries in enumerate(GROUPS[i]):
                 top_each = top[:].unsqueeze(1).to_broadcast(shifted[g][:].shape)
-                nc.tensor.matmul(shifted[g][:], minus_identity[:], top_each, start=False, stop=True)
+                if on_vector:
+                    nc.vector.tensor_tensor(shifted[g][:], logit[i][:, entries, :], top_each, ALU.subtract)
+                else:
+                    nc.tensor.matmul(shifted[g][:], minus_identity[:], top_each, start=False, stop=True)
                 nc.scalar.activation(w[:, entries, PIECES[i]], shifted[g][:], ACT.Exp)
 
         den_four = held.tile([P, QUAD, N], F32, name="den_four")
@@ -162,6 +186,8 @@ def tile_hgnnscheduler_kernel(tc, base, adj, proc, el, er, offs, out):
 
         for i in pieces:
             own_entry(i)
+        for i in pieces:
+            open_banks(i)
         for i in pieces:
             el_and_drop(i)
         for i in pieces:

@@ -41,15 +41,13 @@ def tile_hgnnscheduler_kernel(tc, base, adj, proc, el, er, offs, out):
         nc.sync.dma_start(er_sb[:], er)
         offsets = held.tile([P, N // 16], U16, name="offsets")
         nc.sync.dma_start(offsets[:], offs)
+        el_top = held.tile([P, OPS, N], F32, name="el_top")
+        nc.vector.memset(el_top[:, op_groups[0], :], 0.0)
+        nc.gpsimd.memset(el_top[:, op_groups[1], :], 0.0)
+        nc.sync.dma_start(el_top[0:1, :, :], el_row)
         adj_sb = held.tile([P, OPS, N], F32, name="adj_sb")
         proc_sb = held.tile([P, OPS, N], F32, name="proc_sb")
-        el_top = []
-        for h, ops in zip(range(HALVES), op_groups):
-            columns = slice(h * HALF, (h + 1) * HALF)
-            padded = held.tile([P, OPS, HALF], F32, name=f"el_top{h}")
-            nc.vector.memset(padded[:], 0.0)
-            nc.sync.dma_start(padded[0:1, :, :], el_row[:, :, columns])
-            el_top.append(padded)
+        for ops in op_groups:
             nc.scalar.dma_start(adj_sb[:, ops, :], adj_by_machine[:, ops, :])
             nc.sync.dma_start(proc_sb[:, ops, :], proc_by_machine[:, ops, :])
         windows = []
@@ -106,10 +104,8 @@ def tile_hgnnscheduler_kernel(tc, base, adj, proc, el, er, offs, out):
                 nc.scalar.activation(drop[i][:, ops, :], adj_sb[:, ops, columns], ACT.Copy, bias=-DROP, scale=DROP)
                 first = (i, g) not in er_in_bank
                 nc.tensor.matmul(banks_of[i][g][:], identity[:], drop[i][:, ops, :], start=first, stop=False)
-            half = columns.start // HALF
-            in_half = slice(columns.start - half * HALF, columns.stop - half * HALF)
             for g, entries in enumerate(GROUPS[i]):
-                el_piece = el_top[half][:, operations(entries), in_half]
+                el_piece = el_top[:, operations(entries), columns]
                 nc.tensor.matmul(banks_of[i][g][:], first_row[:], el_piece, start=False, stop=True)
 
         def logits(i):

@@ -56,15 +56,15 @@ def tile_hgnnscheduler_kernel(tc, base, adj, proc, el, er, offs, out):
             nc.sync.dma_start(window[:], base_blocks[n])
             windows.append(window)
 
-        identity_f32 = held.tile([P, P], F32, name="identity_f32")
-        make_identity(nc, identity_f32[:])
-        identity = held.tile([P, P], BF16, name="identity")
-        nc.gpsimd.tensor_scalar_mul(identity[:], identity_f32[:], 1.0)
         first_row = held.tile([P, P], F32, name="first_row")
         nc.gpsimd.memset(first_row[:], 0.0)
         nc.gpsimd.memset(first_row[0:1, :], 1.0)
+        identity = held.tile([P, P], BF16, name="identity")
+        make_identity(nc, identity[:])
+        identity_f32 = held.tile([P, P], F32, name="identity_f32")
+        nc.gpsimd.tensor_copy(identity_f32[:], identity[:])
         minus_identity = held.tile([P, P], BF16, name="minus_identity")
-        nc.gpsimd.tensor_scalar_mul(minus_identity[:], identity_f32[:], -1.0)
+        nc.gpsimd.tensor_scalar_mul(minus_identity[:], identity[:], -1.0)
 
         pieces = range(len(PIECES))
         width = [columns.stop - columns.start for columns in PIECES]
@@ -85,52 +85,38 @@ def tile_hgnnscheduler_kernel(tc, base, adj, proc, el, er, offs, out):
                 logit[i][:, SELF, :], twice_er[:], SLOPE, twice_er[:], ALU.mult, ALU.max
             )
 
-        er_in_bank = [(0, 1)]
         banks_of = [[] for i in pieces]
 
-        def open_banks(i):
+        def open_with_el(i):
             for g, entries in enumerate(GROUPS[i]):
-                shape = score[i][:, operations(entries), :].shape
-                bank = banks.tile(shape, F32, name=f"sum{i}{g}")
-                if (i, g) in er_in_bank:
-                    er_each = er_sb[:, PIECES[i]].unsqueeze(1).to_broadcast(shape)
-                    nc.tensor.matmul(bank[:], identity_f32[:], er_each, start=True, stop=False)
+                el_piece = el_top[:, operations(entries), PIECES[i]]
+                bank = banks.tile(el_piece.shape, F32, name=f"el_drop{i}{g}")
+                nc.tensor.matmul(bank[:], first_row[:], el_piece, start=True, stop=False)
                 banks_of[i].append(bank)
 
-        def el_and_drop(i):
-            columns = PIECES[i]
+        def close_with_drop(i):
             for g, entries in enumerate(GROUPS[i]):
                 ops = operations(entries)
-                nc.scalar.activation(drop[i][:, ops, :], adj_sb[:, ops, columns], ACT.Copy, bias=-DROP, scale=DROP)
-                first = (i, g) not in er_in_bank
-                nc.tensor.matmul(banks_of[i][g][:], identity[:], drop[i][:, ops, :], start=first, stop=False)
-            for g, entries in enumerate(GROUPS[i]):
-                el_piece = el_top[:, operations(entries), columns]
-                nc.tensor.matmul(banks_of[i][g][:], first_row[:], el_piece, start=False, stop=True)
+                adj_piece = adj_sb[:, ops, PIECES[i]]
+                nc.scalar.activation(drop[i][:, ops, :], adj_piece, ACT.Copy, bias=-DROP, scale=DROP)
+                nc.tensor.matmul(banks_of[i][g][:], identity[:], drop[i][:, ops, :], start=False, stop=True)
 
         def logits(i):
             columns = PIECES[i]
             er_piece = er_sb[:, columns]
+            for entries in GROUPS[i]:
+                ops = operations(entries)
+                nc.vector.scalar_tensor_tensor(
+                    score[i][:, ops, :],
+                    proc_sb[:, ops, columns],
+                    KAPPA,
+                    er_piece.unsqueeze(1).to_broadcast(score[i][:, ops, :].shape),
+                    ALU.mult,
+                    ALU.add,
+                )
             for g, entries in enumerate(GROUPS[i]):
                 ops = operations(entries)
-                if (i, g) not in er_in_bank:
-                    nc.vector.scalar_tensor_tensor(
-                        score[i][:, ops, :],
-                        proc_sb[:, ops, columns],
-                        KAPPA,
-                        er_piece.unsqueeze(1).to_broadcast(score[i][:, ops, :].shape),
-                        ALU.mult,
-                        ALU.add,
-                    )
-            for g, entries in enumerate(GROUPS[i]):
-                ops = operations(entries)
-                bank = banks_of[i][g]
-                if (i, g) in er_in_bank:
-                    nc.vector.scalar_tensor_tensor(
-                        score[i][:, ops, :], proc_sb[:, ops, columns], KAPPA, bank[:], ALU.mult, ALU.add
-                    )
-                else:
-                    nc.vector.tensor_tensor(score[i][:, ops, :], score[i][:, ops, :], bank[:], ALU.add)
+                nc.vector.tensor_tensor(score[i][:, ops, :], score[i][:, ops, :], banks_of[i][g][:], ALU.add)
                 nc.vector.scalar_tensor_tensor(
                     logit[i][:, ops, :], score[i][:, ops, :], SLOPE, score[i][:, ops, :], ALU.mult, ALU.max
                 )
@@ -183,9 +169,9 @@ def tile_hgnnscheduler_kernel(tc, base, adj, proc, el, er, offs, out):
         for i in pieces:
             own_entry(i)
         for i in pieces:
-            open_banks(i)
+            open_with_el(i)
         for i in pieces:
-            el_and_drop(i)
+            close_with_drop(i)
         for i in pieces:
             logits(i)
             exponentials(i)

@@ -37,24 +37,29 @@ def tile_hgnnscheduler_kernel(tc, base, adj, proc, el, er, offs, out):
         tc.tile_pool(name="held", bufs=1) as held,
         tc.psum_pool(name="banks", bufs=1) as banks,
     ):
+        el_line = held.tile([1, OPS, N], F32, name="el_line")
+        nc.sync.dma_start(el_line[:], el_row)
         er_sb = held.tile([P, N], F32, name="er_sb")
         nc.sync.dma_start(er_sb[:], er)
-        offsets = held.tile([P, N // 16], U16, name="offsets")
-        nc.sync.dma_start(offsets[:], offs)
-        el_top = held.tile([P, OPS, N], F32, name="el_top")
-        nc.vector.memset(el_top[:, op_groups[0], :], 0.0)
-        nc.gpsimd.memset(el_top[:, op_groups[1], :], 0.0)
-        nc.sync.dma_start(el_top[0:1, :, :], el_row)
         adj_sb = held.tile([P, OPS, N], F32, name="adj_sb")
         proc_sb = held.tile([P, OPS, N], F32, name="proc_sb")
         for ops in op_groups:
             nc.scalar.dma_start(adj_sb[:, ops, :], adj_by_machine[:, ops, :])
             nc.sync.dma_start(proc_sb[:, ops, :], proc_by_machine[:, ops, :])
+        offsets = held.tile([P, N // 16], U16, name="offsets")
+        nc.sync.dma_start(offsets[:], offs)
         windows = []
         for n in range(ENTRIES):
             window = held.tile([P, STORE], F32, name=f"window{n}")
             nc.sync.dma_start(window[:], base_blocks[n])
             windows.append(window)
+
+        el_top = held.tile([P, OPS, N], F32, name="el_top")
+        first_ops, last_ops = op_groups
+        nc.vector.memset(el_top[:, first_ops, :], 0.0)
+        nc.gpsimd.memset(el_top[:, last_ops, :], 0.0)
+        nc.vector.tensor_copy(el_top[0:1, first_ops, :], el_line[:, first_ops, :])
+        nc.scalar.activation(el_top[0:1, last_ops, :], el_line[:, last_ops, :], ACT.Copy)
 
         first_row = held.tile([P, P], F32, name="first_row")
         nc.gpsimd.memset(first_row[:], 0.0)
@@ -87,19 +92,19 @@ def tile_hgnnscheduler_kernel(tc, base, adj, proc, el, er, offs, out):
 
         banks_of = [[] for i in pieces]
 
-        def open_with_el(i):
-            for g, entries in enumerate(GROUPS[i]):
-                el_piece = el_top[:, operations(entries), PIECES[i]]
-                bank = banks.tile(el_piece.shape, F32, name=f"el_drop{i}{g}")
-                nc.tensor.matmul(bank[:], first_row[:], el_piece, start=True, stop=False)
-                banks_of[i].append(bank)
-
-        def close_with_drop(i):
+        def el_and_drop(i):
             for g, entries in enumerate(GROUPS[i]):
                 ops = operations(entries)
                 adj_piece = adj_sb[:, ops, PIECES[i]]
                 nc.scalar.activation(drop[i][:, ops, :], adj_piece, ACT.Copy, bias=-DROP, scale=DROP)
-                nc.tensor.matmul(banks_of[i][g][:], identity[:], drop[i][:, ops, :], start=False, stop=True)
+                bank = banks.tile(adj_piece.shape, F32, name=f"el_drop{i}{g}")
+                el_first = i == 0
+                if el_first:
+                    nc.tensor.matmul(bank[:], first_row[:], el_top[:, ops, PIECES[i]], start=True, stop=False)
+                nc.tensor.matmul(bank[:], identity[:], drop[i][:, ops, :], start=not el_first, stop=el_first)
+                if not el_first:
+                    nc.tensor.matmul(bank[:], first_row[:], el_top[:, ops, PIECES[i]], start=False, stop=True)
+                banks_of[i].append(bank)
 
         def logits(i):
             columns = PIECES[i]
@@ -169,9 +174,7 @@ def tile_hgnnscheduler_kernel(tc, base, adj, proc, el, er, offs, out):
         for i in pieces:
             own_entry(i)
         for i in pieces:
-            open_with_el(i)
-        for i in pieces:
-            close_with_drop(i)
+            el_and_drop(i)
         for i in pieces:
             logits(i)
             exponentials(i)

@@ -168,8 +168,7 @@ def tile_hgnnscheduler_kernel(tc, base, adj, proc, el, er, offs, out):
             nc.vector.reciprocal(inv_den[:, columns], den[:, columns])
 
         def store(n):
-            queue = nc.sync if n % 2 == 0 else nc.scalar
-            queue.dma_start(out_blocks[n], windows[n][:])
+            nc.sync.dma_start(out_blocks[n], windows[n][:])
 
         for i in pieces:
             own_entry(i)

@@ -44,8 +44,8 @@ def tile_hgnnscheduler_kernel(tc, base, adj, proc, el, er, offs, out):
         adj_sb = held.tile([P, OPS, N], F32, name="adj_sb")
         proc_sb = held.tile([P, OPS, N], F32, name="proc_sb")
         for ops in op_groups:
-            nc.scalar.dma_start(adj_sb[:, ops, :], adj_by_machine[:, ops, :])
             nc.sync.dma_start(proc_sb[:, ops, :], proc_by_machine[:, ops, :])
+            nc.sync.dma_start(adj_sb[:, ops, :], adj_by_machine[:, ops, :])
         offsets = held.tile([P, N // 16], U16, name="offsets")
         nc.sync.dma_start(offsets[:], offs)
         windows = []
@@ -58,8 +58,9 @@ def tile_hgnnscheduler_kernel(tc, base, adj, proc, el, er, offs, out):
         first_ops, last_ops = op_groups
         nc.vector.memset(el_top[:, first_ops, :], 0.0)
         nc.gpsimd.memset(el_top[:, last_ops, :], 0.0)
-        nc.vector.tensor_copy(el_top[0:1, first_ops, :], el_line[:, first_ops, :])
-        nc.scalar.activation(el_top[0:1, last_ops, :], el_line[:, last_ops, :], ACT.Copy)
+        for ops in op_groups:
+            nc.vector.tensor_copy(el_top[0:1, ops, 0:HALF], el_line[:, ops, 0:HALF])
+        nc.scalar.activation(el_top[0:1, :, HALF:N], el_line[:, :, HALF:N], ACT.Copy)
 
         first_row = held.tile([P, P], F32, name="first_row")
         nc.gpsimd.memset(first_row[:], 0.0)

import concourse.mybir as mybir
from concourse.masks import make_identity

F32 = mybir.dt.float32
BF16 = mybir.dt.bfloat16
U16 = mybir.dt.uint16
ALU = mybir.AluOpType
ACT = mybir.ActivationFunctionType

P = 128
OPS = 7
SELF = OPS
ENTRIES = OPS + 1
N = 256
HALVES = 2
HALF = N // HALVES
STORE = 1024
KAPPA = 1.5
SLOPE = 0.2
DROP = 32768.0
QUAD = 4
QUARTER = N // 4
PIECES = [slice(0, HALF), slice(HALF, HALF + QUARTER), slice(HALF + QUARTER, N)]
GROUPS = [[slice(0, QUAD), slice(QUAD, ENTRIES)], [slice(0, ENTRIES)], [slice(0, ENTRIES)]]


def tile_hgnnscheduler_kernel(tc, base, adj, proc, el, er, offs, out):
    nc = tc.nc
    base_blocks = base.rearrange("(n p) s -> n p s", p=P)
    out_blocks = out.rearrange("(n p) s -> n p s", p=P)
    proc_by_machine = proc.rearrange("(n p) j -> p n j", p=P)
    adj_by_machine = adj.rearrange("(n p) j -> p n j", p=P)
    el_row = el.rearrange("(a n) j -> a n j", a=1)
    op_groups = [slice(0, QUAD), slice(QUAD, OPS)]

    with (
        tc.tile_pool(name="held", bufs=1) as held,
        tc.psum_pool(name="banks", bufs=1) as banks,
    ):
        el_line = held.tile([1, OPS, N], F32, name="el_line")
        nc.sync.dma_start(el_line[:], el_row)
        er_sb = held.tile([P, N], F32, name="er_sb")
        nc.sync.dma_start(er_sb[:], er)
        adj_sb = held.tile([P, OPS, N], F32, name="adj_sb")
        proc_sb = held.tile([P, OPS, N], F32, name="proc_sb")
        for ops in op_groups:
            nc.sync.dma_start(proc_sb[:, ops, :], proc_by_machine[:, ops, :])
            nc.sync.dma_start(adj_sb[:, ops, :], adj_by_machine[:, ops, :])
        offsets = held.tile([P, N // 16], U16, name="offsets")
        nc.sync.dma_start(offsets[:], offs)
        windows = []
        for n in range(ENTRIES):
            window = held.tile([P, STORE], F32, name=f"window{n}")
            nc.sync.dma_start(window[:], base_blocks[n])
            windows.append(window)

        el_top = held.tile([P, OPS, N], F32, name="el_top")
        first_ops, last_ops = op_groups
        nc.vector.memset(el_top[:, first_ops, :], 0.0)
        nc.gpsimd.memset(el_top[:, last_ops, :], 0.0)
        for ops in op_groups:
            nc.vector.tensor_copy(el_top[0:1, ops, 0:HALF], el_line[:, ops, 0:HALF])
        nc.scalar.activation(el_top[0:1, :, HALF:N], el_line[:, :, HALF:N], ACT.Copy)

        first_row = held.tile([P, P], F32, name="first_row")
        nc.gpsimd.memset(first_row[:], 0.0)
        nc.gpsimd.memset(first_row[0:1, :], 1.0)
        identity = held.tile([P, P], BF16, name="identity")
        make_identity(nc, identity[:])
        identity_f32 = held.tile([P, P], F32, name="identity_f32")
        nc.gpsimd.tensor_copy(identity_f32[:], identity[:])
        minus_identity = held.tile([P, P], BF16, name="minus_identity")
        nc.gpsimd.tensor_scalar_mul(minus_identity[:], identity[:], -1.0)

        pieces = range(len(PIECES))
        width = [columns.stop - columns.start for columns in PIECES]
        drop = [held.tile([P, OPS, width[i]], BF16, name=f"drop{i}") for i in pieces]
        score = [held.tile([P, OPS, width[i]], F32, name=f"score{i}") for i in pieces]
        logit = [held.tile([P, ENTRIES, width[i]], F32, name=f"logit{i}") for i in pieces]
        w = held.tile([P, ENTRIES, N], F32, name="w")
        inv_den = held.tile([P, N], F32, name="inv_den")

        def operations(entries):
            return slice(entries.start, min(entries.stop, OPS))

        def own_entry(i):
            er_piece = er_sb[:, PIECES[i]]
            twice_er = held.tile([P, width[i]], F32, name=f"twice_er{i}")
            nc.vector.tensor_tensor(twice_er[:], er_piece, er_piece, ALU.add)
            nc.vector.scalar_tensor_tensor(
                logit[i][:, SELF, :], twice_er[:], SLOPE, twice_er[:], ALU.mult, ALU.max
            )

        banks_of = [[] for i in pieces]

        def el_and_drop(i):
            for g, entries in enumerate(GROUPS[i]):
                ops = operations(entries)
                adj_piece = adj_sb[:, ops, PIECES[i]]
                nc.scalar.activation(drop[i][:, ops, :], adj_piece, ACT.Copy, bias=-DROP, scale=DROP)
                bank = banks.tile(adj_piece.shape, F32, name=f"el_drop{i}{g}")
                el_first = i == 0
                if el_first:
                    nc.tensor.matmul(bank[:], first_row[:], el_top[:, ops, PIECES[i]], start=True, stop=False)
                nc.tensor.matmul(bank[:], identity[:], drop[i][:, ops, :], start=not el_first, stop=el_first)
                if not el_first:
                    nc.tensor.matmul(bank[:], first_row[:], el_top[:, ops, PIECES[i]], start=False, stop=True)
                banks_of[i].append(bank)

        def logits(i):
            columns = PIECES[i]
            er_piece = er_sb[:, columns]
            for entries in GROUPS[i]:
                ops = operations(entries)
                nc.vector.scalar_tensor_tensor(
                    score[i][:, ops, :],
                    proc_sb[:, ops, columns],
                    KAPPA,
                    er_piece.unsqueeze(1).to_broadcast(score[i][:, ops, :].shape),
                    ALU.mult,
                    ALU.add,
                )
            for g, entries in enumerate(GROUPS[i]):
                ops = operations(entries)
                nc.vector.tensor_tensor(score[i][:, ops, :], score[i][:, ops, :], banks_of[i][g][:], ALU.add)
                nc.vector.scalar_tensor_tensor(
                    logit[i][:, ops, :], score[i][:, ops, :], SLOPE, score[i][:, ops, :], ALU.mult, ALU.max
                )

        def exponentials(i):
            on_vector = i == 1
            shifted = []
            for g, entries in enumerate(GROUPS[i]):
                if on_vector:
                    below_top = held.tile(logit[i][:, entries, :].shape, F32, name=f"below_top{i}{g}")
                    shifted.append(below_top)
                else:
                    bank = banks.tile(logit[i][:, entries, :].shape, F32, name=f"shifted{i}{g}")
                    nc.tensor.matmul(bank[:], identity_f32[:], logit[i][:, entries, :], start=True, stop=False)
                    shifted.append(bank)
            top_four = held.tile([P, QUAD, width[i]], BF16, name=f"top_four{i}")
            nc.vector.tensor_tensor(top_four[:], logit[i][:, 0:QUAD, :], logit[i][:, QUAD:ENTRIES, :], ALU.max)
            top_two = held.tile([P, 2, width[i]], BF16, name=f"top_two{i}")
            nc.vector.tensor_tensor(top_two[:], top_four[:, 0:2, :], top_four[:, 2:4, :], ALU.max)
            top = held.tile([P, width[i]], BF16, name=f"top{i}")
            nc.vector.tensor_tensor(top[:], top_two[:, 0, :], top_two[:, 1, :], ALU.max)
            for g, entries in enumerate(GROUPS[i]):
                top_each = top[:].unsqueeze(1).to_broadcast(shifted[g][:].shape)
                if on_vector:
                    nc.vector.tensor_tensor(shifted[g][:], logit[i][:, entries, :], top_each, ALU.subtract)
                else:
                    nc.tensor.matmul(shifted[g][:], minus_identity[:], top_each, start=False, stop=True)
                nc.scalar.activation(w[:, entries, PIECES[i]], shifted[g][:], ACT.Exp)

        den_four = held.tile([P, QUAD, N], F32, name="den_four")
        den_two = held.tile([P, 2, N], F32, name="den_two")
        den = held.tile([P, N], F32, name="den")

        def add_to_four(columns):
            nc.vector.tensor_tensor(den_four[:, :, columns], w[:, 0:QUAD, columns], w[:, QUAD:ENTRIES, columns], ALU.add)

        def add_to_two(columns):
            nc.vector.tensor_tensor(den_two[:, :, columns], den_four[:, 0:2, columns], den_four[:, 2:4, columns], ALU.add)

        def add_to_one(columns):
            nc.vector.tensor_tensor(den[:, columns], den_two[:, 0, columns], den_two[:, 1, columns], ALU.add)

        def invert(columns):
            nc.vector.reciprocal(inv_den[:, columns], den[:, columns])

        def store(n):
            nc.sync.dma_start(out_blocks[n], windows[n][:])

        for i in pieces:
            own_entry(i)
        for i in pieces:
            el_and_drop(i)
        for i in pieces:
            logits(i)
            exponentials(i)
        for step in (add_to_four, add_to_two, add_to_one, invert):
            for columns in PIECES:
                step(columns)

        for n in range(ENTRIES):
            nc.vector.tensor_tensor(windows[n][:].indirect(offsets[:]), w[:, n, :], inv_den[:], ALU.mult)
            store(n)
